import numpy as np
import ml_dtypes


def mxq(x, axis, fmt="e4m3"):
    dtype, down = {"e4m3": (ml_dtypes.float8_e4m3fn, 7), "e5m2": (ml_dtypes.float8_e5m2, 14)}[fmt]
    v = np.moveaxis(np.asarray(x, np.float32).astype(ml_dtypes.bfloat16).astype(np.float64), axis, -1)
    blocks = v.reshape(v.shape[:-1] + (-1, 32))
    amax = np.abs(blocks).max(-1, keepdims=True)
    byte = np.maximum(np.where(amax > 0, np.frexp(amax)[1] - 1 + 127, 0) - down, 1)
    scale = np.exp2(byte - 127.0)
    codes = (blocks / scale).astype(np.float32).astype(dtype).astype(np.float64)
    return np.moveaxis((codes * scale).reshape(v.shape), -1, axis)


WIDE = False


def mx_kscale(k):
    if not WIDE:
        return np.ones(k)
    levels = np.array([10, -10, 5, -5, 0])
    if k % 512:
        return np.exp2(np.random.permutation(np.resize(levels, k // 32))).repeat(32)
    a = np.empty((k // 512, 16))
    for p in range(k // 512):
        a[p, :8] = np.random.permutation(np.resize(levels, 8))
        for g in range(8):
            far = levels[np.abs(levels - a[p, g]) >= 10]
            a[p, g + 8] = far[np.random.randint(len(far))]
    return np.exp2(a.ravel()).repeat(32)


BF16 = ml_dtypes.bfloat16


def bf(x):
    return np.asarray(x, np.float32).astype(BF16)


def f64(x):
    return np.asarray(x).astype(np.float64)


T, HS, WS, WT, WH, WW, NH, HD, VID_DIM, TXT_DIM, TXT_LEN = 8, 8, 16, 8, 8, 8, 8, 128, 1536, 1536, 256
EPS = 1e-6
L_VID = T * HS * WS
N_WIN = (T // WT) * (HS // WH) * (WS // WW)
WIN_LEN = WT * WH * WW
INNER = NH * HD


def rmsnorm(x, gain):
    return x * (1.0 / np.sqrt(np.mean(x * x, axis=-1, keepdims=True) + EPS)) * gain


def window_partition(x):
    x = x.reshape(T // WT, WT, HS // WH, WH, WS // WW, WW, NH, HD)
    x = x.transpose(0, 2, 4, 1, 3, 5, 6, 7)
    return x.reshape(N_WIN, WIN_LEN, NH, HD)


def draw0():
    s = mx_kscale(VID_DIM)
    return {
        "vid": bf(np.random.standard_normal((L_VID, VID_DIM)) * s),
        "Wqkv_vid": bf(np.random.standard_normal((VID_DIM, 3 * INNER)) / np.sqrt(VID_DIM) / s[:, None]),
        "bqkv_vid": bf(0.1 * np.random.standard_normal(3 * INNER)),
        "q_scale_vid": bf(1.0 + 0.1 * np.random.standard_normal(HD)),
        "k_scale_vid": bf(1.0 + 0.1 * np.random.standard_normal(HD)),
    }


def core(vid, Wqkv_vid, bqkv_vid, q_scale_vid, k_scale_vid):
    qkv = ((mxq(f64(vid), 1, "e4m3") @ mxq(f64(Wqkv_vid), 0, "e4m3")) + f64(bqkv_vid)).reshape(L_VID, 3, NH, HD)
    q = rmsnorm(qkv[:, 0], f64(q_scale_vid))
    k = rmsnorm(qkv[:, 1], f64(k_scale_vid))
    return window_partition(q), window_partition(k), window_partition(qkv[:, 2])


def e4m3fn_bytes(y):
    return np.clip(np.asarray(y, np.float64), -448.0, 448.0).astype(np.float32).astype(ml_dtypes.float8_e4m3fn).view(np.uint8)


def e4m3fn_values(b):
    return np.asarray(b, np.uint8).view(ml_dtypes.float8_e4m3fn).astype(np.float64)


def setup_inputs():
    d = draw0()
    x0 = np.asarray(d['Wqkv_vid']).astype(np.float64)
    s = (np.max(np.abs(x0), axis=(1,), keepdims=True) / 448.0).astype(np.float32)
    out = {}
    for k, v in d.items():
        if k == 'Wqkv_vid':
            out['Wqkv_vid_bytes'] = e4m3fn_bytes(x0 / s.astype(np.float64))
            out['Wqkv_vid_scale'] = s
        else:
            out[k] = v
    return out


def reference(vid, Wqkv_vid_bytes, Wqkv_vid_scale, bqkv_vid, q_scale_vid, k_scale_vid):
    return core(vid, e4m3fn_values(Wqkv_vid_bytes) * Wqkv_vid_scale.astype(np.float64), bqkv_vid, q_scale_vid, k_scale_vid)

@@ -1,0 +1,265 @@
+from contextlib import ExitStack
+
+import concourse.mybir as mybir
+from concourse.masks import make_identity
+
+F32 = mybir.dt.float32
+BF16 = mybir.dt.bfloat16
+U32 = mybir.dt.uint32
+U8 = mybir.dt.uint8
+FP8 = mybir.dt.float8_e4m3fn
+FP8X4 = mybir.dt.float8_e4m3fn_x4
+ACT = mybir.ActivationFunctionType
+ALU = mybir.AluOpType
+
+P = 128
+TOKENS, K, N = 1024, 1536, 3072
+PASSES = 3
+CHUNK = 512
+NCHUNK = 6
+HD = 128
+EPS = 1e-6
+FLOPS = 2 * TOKENS * K * N
+
+WIDEN_ON_V = {(0, 1, 0), (0, 1, 1), (0, 1, 2), (0, 1, 3)}
+INTER_ON_S_G = (2,)
+EVAC_ON_S_G = (2,)
+
+
+def tile_naswinattention_pa_kernel(
+    tc, vid, w_bytes, w_scale, bias, q_gain, k_gain, out_q, out_k, out_v
+):
+    nc = tc.nc
+    with ExitStack() as ctx:
+        keep = ctx.enter_context(tc.tile_pool(name="keep", bufs=1))
+        vrawp = ctx.enter_context(tc.tile_pool(name="vrawp", bufs=8))
+        widep = ctx.enter_context(tc.tile_pool(name="widep", bufs=4))
+        grpp = ctx.enter_context(tc.tile_pool(name="grpp", bufs=3))
+        vgp = ctx.enter_context(tc.tile_pool(name="vgp", bufs=4))
+        yp = ctx.enter_context(tc.tile_pool(name="yp", bufs=12))
+        statp = ctx.enter_context(tc.tile_pool(name="statp", bufs=8))
+        junkp = ctx.enter_context(tc.tile_pool(name="junkp", bufs=2))
+        psum = ctx.enter_context(tc.psum_pool(name="psum", bufs=8))
+
+        wsc = keep.tile([P, PASSES, 4], F32, name="wsc")
+        wbytes = keep.tile([P, PASSES, NCHUNK, 4, CHUNK], U8, name="wbytes")
+        wcodes = keep.tile([P, PASSES, N], U32, name="wcodes", align_bytes=64)
+        wscl = keep.tile([P, PASSES, N], U8, name="wscl", align_bytes=64)
+        vcodes = keep.tile([P, 12, 2, P], U32, name="vcodes", align_bytes=64)
+        vscl = keep.tile([P, 12, 2, P], U8, name="vscl", align_bytes=64)
+        bias_bc = keep.tile([P, N], BF16, name="bias_bc")
+        gq = keep.tile([P, HD], BF16, name="gq")
+        gk = keep.tile([P, HD], BF16, name="gk")
+        ident = keep.tile([P, P], F32, name="ident")
+        perm = keep.tile([P, P], F32, name="perm")
+        eps_t = keep.tile([P, 1], F32, name="eps_t")
+        warm = keep.tile([P, 1], F32, name="warm")
+
+        w_view = w_bytes.rearrange("(g p t) n -> g p t n", p=P, t=4)
+
+        def load_w(c, g):
+            nc.sync.dma_start(
+                out=wbytes[:, g, c, :, :],
+                in_=w_view[g, :, :, c * CHUNK : (c + 1) * CHUNK],
+            )
+
+        vraw = []
+
+        def load_vid(a):
+            t = vrawp.tile([P, K], BF16, name="vraw", tag="vraw")
+            nc.sync.dma_start(out=t[:], in_=vid[a * P : (a + 1) * P, :])
+            vraw.append(t)
+
+        nc.sync.dma_start(
+            out=wsc[:], in_=w_scale.rearrange("(g p t) o -> p g (t o)", p=P, t=4)
+        )
+        load_w(0, 0)
+        load_vid(0)
+        load_vid(1)
+        load_w(0, 1)
+        load_w(0, 2)
+        for a in range(2, 8):
+            load_vid(a)
+        for g in range(PASSES):
+            load_w(1, g)
+        nc.sync.dma_start(out=bias_bc[:], in_=bias.partition_broadcast(P))
+        nc.sync.dma_start(out=gq[:], in_=q_gain.partition_broadcast(P))
+        nc.sync.dma_start(out=gk[:], in_=k_gain.partition_broadcast(P))
+        for c in range(2, NCHUNK):
+            for g in range(PASSES):
+                load_w(c, g)
+
+        nc.vector.memset(eps_t[:], EPS)
+        nc.scalar.activation(out=warm[:], in_=eps_t[:], func=ACT.Sqrt)
+        make_identity(nc, ident[:])
+        nc.vector.tensor_copy(
+            out=perm[:].rearrange("p (n h w) -> p n h w", n=2, h=8, w=8),
+            in_=ident[:].rearrange("p (h n w) -> p n h w", h=8, n=2, w=8),
+        )
+
+        wide_of = {}
+        grp_of = {}
+
+        def widen(c, g, t):
+            if t == 0:
+                wide_of[(c, g)] = widep.tile([P, 4, CHUNK], BF16, name="wide", tag="wide")
+            wide = wide_of[(c, g)]
+            src = wbytes[:, g, c, t, :].bitcast(FP8)
+            if (c, g, t) in WIDEN_ON_V:
+                nc.vector.tensor_scalar(
+                    out=wide[:, t, :], in0=src, scalar1=wsc[:, g, t : t + 1],
+                    scalar2=None, op0=ALU.mult,
+                )
+            else:
+                nc.scalar.activation(
+                    out=wide[:, t, :], in_=src, func=ACT.Copy, scale=wsc[:, g, t : t + 1]
+                )
+
+        def interleave(c, g):
+            grp = grpp.tile([P, CHUNK, 4], BF16, name="grp", tag="grp", align_bytes=64)
+            grp_of[(c, g)] = grp
+            src = wide_of[(c, g)][:].rearrange("p t n -> p n t")
+            if g in INTER_ON_S_G:
+                nc.scalar.copy(out=grp[:], in_=src)
+            else:
+                nc.vector.tensor_copy(out=grp[:], in_=src)
+
+        def quant_w(c, g):
+            cols = slice(c * CHUNK, (c + 1) * CHUNK)
+            nc.vector.quantize_mx(
+                out=wcodes[:, g, cols].bitcast(FP8X4),
+                scales=wscl[:, g, cols],
+                in_=grp_of[(c, g)][:].rearrange("p n t -> p (n t)"),
+            )
+
+        def prep_items(c):
+            items = []
+            for g in range(PASSES):
+                for t in range(4):
+                    items.append(lambda c=c, g=g, t=t: widen(c, g, t))
+                items.append(lambda c=c, g=g: interleave(c, g))
+                items.append(lambda c=c, g=g: quant_w(c, g))
+            return items
+
+        def vid_unit(j, g):
+            unit = j * PASSES + g
+            xt = psum.tile([P, 2, 2, P], F32, name="xt", tag="bank")
+            for a2 in range(2):
+                words = vraw[2 * j + a2][:].bitcast(F32)
+                for u in range(2):
+                    nc.tensor.transpose(
+                        xt[:, a2, u, :],
+                        words[:, 256 * g + u : 256 * (g + 1) : 2],
+                        perm[:],
+                    )
+            vg = vgp.tile([P, 2, 256], F32, name="vg", tag="vg", align_bytes=64)
+            for n in range(2):
+                dst = vg[:, n, :].rearrange("p (a c u) -> p a c u", a=2, c=64, u=2)
+                src = xt[:, :, :, n * 64 : (n + 1) * 64].rearrange("p a u c -> p a c u")
+                if g in EVAC_ON_S_G:
+                    nc.scalar.copy(out=dst, in_=src)
+                else:
+                    nc.vector.tensor_copy(out=dst, in_=src)
+            nc.vector.quantize_mx(
+                out=vcodes[:, unit, :, :].rearrange("p n c -> p (n c)").bitcast(FP8X4),
+                scales=vscl[:, unit, :, :].rearrange("p n c -> p (n c)"),
+                in_=vg[:].rearrange("p n w -> p (n w)").bitcast(BF16),
+            )
+
+        acc_of = {}
+        y_of = {}
+        ss_of = {}
+        rt_of = {}
+        outs = (out_q, out_k, out_v)
+        gains = (gq, gk)
+
+        def mm(c, m):
+            j, n = m // 2, m % 2
+            cols = slice(c * CHUNK, (c + 1) * CHUNK)
+            acc = psum.tile([P, CHUNK], F32, name="acc", tag="bank")
+            acc_of[(c, m)] = acc
+            for g in range(PASSES):
+                unit = j * PASSES + g
+                nc.tensor.matmul_mx(
+                    out=acc[:],
+                    lhsT=vcodes[:, unit, n, :].bitcast(FP8X4),
+                    lhsT_scale=vscl[:, unit, n, :],
+                    rhs=wcodes[:, g, cols].bitcast(FP8X4),
+                    rhs_scale=wscl[:, g, cols],
+                    start=(g == 0),
+                    stop=(g == PASSES - 1),
+                )
+
+        def e1(c, m):
+            y = yp.tile([P, CHUNK], F32, name="y", tag="y")
+            y_of[(c, m)] = y
+            nc.vector.tensor_tensor(
+                out=y[:], in0=acc_of[(c, m)][:],
+                in1=bias_bc[:, c * CHUNK : (c + 1) * CHUNK], op=ALU.add,
+            )
+
+        def e2(c, m):
+            y = y_of[(c, m)]
+            ss = statp.tile([P, 4], F32, name="ss", tag="ss")
+            for h in range(4):
+                junk = junkp.tile([P, HD], BF16, name="junk", tag="junk")
+                nc.scalar.activation(
+                    out=junk[:], in_=y[:, h * HD : (h + 1) * HD], func=ACT.Square,
+                    accum_out=ss[:, h : h + 1],
+                )
+            rt = statp.tile([P, 4], F32, name="rt", tag="rt")
+            rt_of[(c, m)] = rt
+            nc.scalar.activation(
+                out=rt[:], in_=ss[:], func=ACT.Sqrt, bias=eps_t[:], scale=1.0 / HD
+            )
+
+        def e3(c, m):
+            y = y_of[(c, m)]
+            rstd = statp.tile([P, 4], F32, name="rstd", tag="rstd")
+            nc.vector.reciprocal(out=rstd[:], in_=rt_of[(c, m)][:])
+            for h in range(4):
+                hs = slice(h * HD, (h + 1) * HD)
+                nc.vector.scalar_tensor_tensor(
+                    out=y[:, hs], in0=y[:, hs], scalar=rstd[:, h : h + 1],
+                    in1=gains[c // 2][:], op0=ALU.mult, op1=ALU.mult,
+                )
+
+        def store(c, m):
+            j, n = m // 2, m % 2
+            half = c % 2
+            view = outs[c // 2].rearrange("n (j c) h d -> n j c (h d)", c=P)
+            nc.sync.dma_start(
+                out=view[n, j, :, half * CHUNK : (half + 1) * CHUNK], in_=y_of[(c, m)][:]
+            )
+
+        for it in prep_items(0):
+            it()
+        for j in range(4):
+            for g in range(PASSES):
+                vid_unit(j, g)
+            mm(0, 2 * j)
+            mm(0, 2 * j + 1)
+
+        for c in range(NCHUNK):
+            items = prep_items(c + 1) if c + 1 < NCHUNK else []
+            normed = c // 2 < 2
+            pos = 0
+            for m in range(8):
+                e1(c, m)
+                if normed:
+                    e2(c, m)
+                else:
+                    store(c, m)
+                upto = min(len(items), ((m + 1) * len(items) + 7) // 8)
+                while pos < upto:
+                    items[pos]()
+                    pos += 1
+                if normed and m >= 1:
+                    e3(c, m - 1)
+                    store(c, m - 1)
+            if normed:
+                e3(c, 7)
+                store(c, 7)
+            if c + 1 < NCHUNK:
+                for m in range(8):
+                    mm(c + 1, m)

@@ -20,10 +20,21 @@ NCHUNK = 6
 HD = 128
 EPS = 1e-6
 FLOPS = 2 * TOKENS * K * N
+NB = 48
+NUNIT = 18
 
-WIDEN_ON_V = {(0, 1, 0), (0, 1, 1), (0, 1, 2), (0, 1, 3)}
-INTER_ON_S_G = (2,)
-EVAC_ON_S_G = (2,)
+LEAD = 3
+E3_LAG = 3
+USE_G = False
+GAIN_PSUM = False
+RSQRT_ON_S = True
+INTER = {}
+INTER_DEFAULT = "V"
+WIDEN_V = {(1, 0), (1, 1), (1, 2), (1, 3)}
+EVAC_V = set()
+DUE_SHIFT = -4
+FAST_INTER = False
+IOFF = {"V": 1, "S": 3, "G": 3}
 
 
 def tile_naswinattention_pa_kernel(
@@ -35,11 +46,15 @@ def tile_naswinattention_pa_kernel(
         vrawp = ctx.enter_context(tc.tile_pool(name="vrawp", bufs=8))
         widep = ctx.enter_context(tc.tile_pool(name="widep", bufs=4))
         grpp = ctx.enter_context(tc.tile_pool(name="grpp", bufs=3))
-        vgp = ctx.enter_context(tc.tile_pool(name="vgp", bufs=4))
+        grpg = ctx.enter_context(tc.tile_pool(name="grpg", bufs=1))
+        vgp = ctx.enter_context(tc.tile_pool(name="vgp", bufs=6))
         yp = ctx.enter_context(tc.tile_pool(name="yp", bufs=12))
         statp = ctx.enter_context(tc.tile_pool(name="statp", bufs=8))
         junkp = ctx.enter_context(tc.tile_pool(name="junkp", bufs=2))
-        psum = ctx.enter_context(tc.psum_pool(name="psum", bufs=8))
+        xtp = ctx.enter_context(tc.psum_pool(name="xtp", bufs=3))
+        accp = ctx.enter_context(tc.psum_pool(name="accp", bufs=4 if GAIN_PSUM else 5))
+        gpp = ctx.enter_context(tc.psum_pool(name="gpp", bufs=1))
+        ctx.enter_context(tc.manual_schedule())
 
         wsc = keep.tile([P, PASSES, 4], F32, name="wsc")
         wbytes = keep.tile([P, PASSES, NCHUNK, 4, CHUNK], U8, name="wbytes")
@@ -48,8 +63,7 @@ def tile_naswinattention_pa_kernel(
         vcodes = keep.tile([P, 12, 2, P], U32, name="vcodes", align_bytes=64)
         vscl = keep.tile([P, 12, 2, P], U8, name="vscl", align_bytes=64)
         bias_bc = keep.tile([P, N], BF16, name="bias_bc")
-        gq = keep.tile([P, HD], BF16, name="gq")
-        gk = keep.tile([P, HD], BF16, name="gk")
+        g_bc = keep.tile([P, 2, HD], BF16, name="g_bc")
         ident = keep.tile([P, P], F32, name="ident")
         perm = keep.tile([P, P], F32, name="perm")
         eps_t = keep.tile([P, 1], F32, name="eps_t")
@@ -74,38 +88,55 @@ def tile_naswinattention_pa_kernel(
             out=wsc[:], in_=w_scale.rearrange("(g p t) o -> p g (t o)", p=P, t=4)
         )
         load_w(0, 0)
-        load_vid(0)
-        load_vid(1)
         load_w(0, 1)
         load_w(0, 2)
-        for a in range(2, 8):
+        for a in range(4):
             load_vid(a)
-        for g in range(PASSES):
-            load_w(1, g)
+        load_w(1, 0)
         nc.sync.dma_start(out=bias_bc[:], in_=bias.partition_broadcast(P))
-        nc.sync.dma_start(out=gq[:], in_=q_gain.partition_broadcast(P))
-        nc.sync.dma_start(out=gk[:], in_=k_gain.partition_broadcast(P))
+        nc.sync.dma_start(out=g_bc[:, 0, :], in_=q_gain.partition_broadcast(P))
+        nc.sync.dma_start(out=g_bc[:, 1, :], in_=k_gain.partition_broadcast(P))
+        load_vid(4)
+        load_vid(5)
+        load_w(1, 1)
+        load_vid(6)
+        load_vid(7)
+        load_w(1, 2)
         for c in range(2, NCHUNK):
             for g in range(PASSES):
                 load_w(c, g)
 
         nc.vector.memset(eps_t[:], EPS)
-        nc.scalar.activation(out=warm[:], in_=eps_t[:], func=ACT.Sqrt)
+        rfunc = ACT.Abs_reciprocal_sqrt if RSQRT_ON_S else ACT.Sqrt
+        nc.scalar.activation(out=warm[:], in_=eps_t[:], func=rfunc)
         make_identity(nc, ident[:])
         nc.vector.tensor_copy(
             out=perm[:].rearrange("p (n h w) -> p n h w", n=2, h=8, w=8),
             in_=ident[:].rearrange("p (h n w) -> p n h w", h=8, n=2, w=8),
         )
 
+        g_ps = None
+        if GAIN_PSUM:
+            ident_bf = keep.tile([P, P], BF16, name="ident_bf")
+            nc.vector.tensor_copy(out=ident_bf[:], in_=ident[:])
+            g_ps = gpp.tile([P, 2, HD], F32, name="g_ps")
+
+        def gains_to_psum():
+            nc.tensor.matmul(
+                out=g_ps[:].rearrange("p a d -> p (a d)"), lhsT=ident_bf[:],
+                rhs=g_bc[:].rearrange("p a d -> p (a d)"), start=True, stop=True,
+            )
+
         wide_of = {}
         grp_of = {}
 
-        def widen(c, g, t):
-            if t == 0:
-                wide_of[(c, g)] = widep.tile([P, 4, CHUNK], BF16, name="wide", tag="wide")
-            wide = wide_of[(c, g)]
+        def widen(x, t):
+            c, g = x // PASSES, x % PASSES
+            if x not in wide_of:
+                wide_of[x] = widep.tile([P, 4, CHUNK], BF16, name="wide", tag="wide")
+            wide = wide_of[x]
             src = wbytes[:, g, c, t, :].bitcast(FP8)
-            if (c, g, t) in WIDEN_ON_V:
+            if (x, t) in WIDEN_V:
                 nc.vector.tensor_scalar(
                     out=wide[:, t, :], in0=src, scalar1=wsc[:, g, t : t + 1],
                     scalar2=None, op0=ALU.mult,
@@ -115,35 +146,43 @@ def tile_naswinattention_pa_kernel(
                     out=wide[:, t, :], in_=src, func=ACT.Copy, scale=wsc[:, g, t : t + 1]
                 )
 
-        def interleave(c, g):
-            grp = grpp.tile([P, CHUNK, 4], BF16, name="grp", tag="grp", align_bytes=64)
-            grp_of[(c, g)] = grp
-            src = wide_of[(c, g)][:].rearrange("p t n -> p n t")
-            if g in INTER_ON_S_G:
-                nc.scalar.copy(out=grp[:], in_=src)
+        def interleave(x):
+            eng = INTER.get(x, INTER_DEFAULT)
+            if eng == "G":
+                grp = grpg.tile([P, CHUNK, 4], BF16, name="grpg", tag="grpg", align_bytes=64)
             else:
-                nc.vector.tensor_copy(out=grp[:], in_=src)
+                grp = grpp.tile([P, CHUNK, 4], BF16, name="grp", tag="grp", align_bytes=64)
+            grp_of[x] = grp
+            if FAST_INTER:
+                dst = grp[:].rearrange("p (c i) t -> p c t i", i=4)
+                src = wide_of[x][:].rearrange("p t (c i) -> p c t i", i=4)
+            else:
+                dst = grp[:]
+                src = wide_of[x][:].rearrange("p t n -> p n t")
+            if eng == "S":
+                nc.scalar.copy(out=dst, in_=src)
+            elif eng == "G":
+                nc.gpsimd.tensor_scalar(
+                    out=dst, in0=src, scalar1=1.0, scalar2=0.0, op0=ALU.mult, op1=ALU.add
+                )
+            else:
+                nc.vector.tensor_copy(out=dst, in_=src)
 
-        def quant_w(c, g):
+        def quant_w(x):
+            c, g = x // PASSES, x % PASSES
             cols = slice(c * CHUNK, (c + 1) * CHUNK)
             nc.vector.quantize_mx(
                 out=wcodes[:, g, cols].bitcast(FP8X4),
                 scales=wscl[:, g, cols],
-                in_=grp_of[(c, g)][:].rearrange("p n t -> p (n t)"),
+                in_=grp_of[x][:].rearrange("p n t -> p (n t)"),
             )
 
-        def prep_items(c):
-            items = []
-            for g in range(PASSES):
-                for t in range(4):
-                    items.append(lambda c=c, g=g, t=t: widen(c, g, t))
-                items.append(lambda c=c, g=g: interleave(c, g))
-                items.append(lambda c=c, g=g: quant_w(c, g))
-            return items
+        xt_of = {}
+        vg_of = {}
 
-        def vid_unit(j, g):
-            unit = j * PASSES + g
-            xt = psum.tile([P, 2, 2, P], F32, name="xt", tag="bank")
+        def vid_t(j, g):
+            xt = xtp.tile([P, 2, 2, P], F32, name="xt", tag="xt")
+            xt_of[(j, g)] = xt
             for a2 in range(2):
                 words = vraw[2 * j + a2][:].bitcast(F32)
                 for u in range(2):
@@ -152,32 +191,42 @@ def tile_naswinattention_pa_kernel(
                         words[:, 256 * g + u : 256 * (g + 1) : 2],
                         perm[:],
                     )
+
+        def vid_x(j, g):
+            xt = xt_of[(j, g)]
             vg = vgp.tile([P, 2, 256], F32, name="vg", tag="vg", align_bytes=64)
+            vg_of[(j, g)] = vg
             for n in range(2):
                 dst = vg[:, n, :].rearrange("p (a c u) -> p a c u", a=2, c=64, u=2)
                 src = xt[:, :, :, n * 64 : (n + 1) * 64].rearrange("p a u c -> p a c u")
-                if g in EVAC_ON_S_G:
-                    nc.scalar.copy(out=dst, in_=src)
-                else:
+                if (j, g) in EVAC_V:
                     nc.vector.tensor_copy(out=dst, in_=src)
+                else:
+                    nc.scalar.copy(out=dst, in_=src)
+
+        def vid_q(j, g):
+            unit = j * PASSES + g
             nc.vector.quantize_mx(
                 out=vcodes[:, unit, :, :].rearrange("p n c -> p (n c)").bitcast(FP8X4),
                 scales=vscl[:, unit, :, :].rearrange("p n c -> p (n c)"),
-                in_=vg[:].rearrange("p n w -> p (n w)").bitcast(BF16),
+                in_=vg_of[(j, g)][:].rearrange("p n w -> p (n w)").bitcast(BF16),
             )
 
         acc_of = {}
         y_of = {}
         ss_of = {}
-        rt_of = {}
+        rs_of = {}
         outs = (out_q, out_k, out_v)
-        gains = (gq, gk)
 
-        def mm(c, m):
+        def normed(b):
+            return 0 <= b < 32
+
+        def mm(b):
+            c, m = b // 8, b % 8
             j, n = m // 2, m % 2
             cols = slice(c * CHUNK, (c + 1) * CHUNK)
-            acc = psum.tile([P, CHUNK], F32, name="acc", tag="bank")
-            acc_of[(c, m)] = acc
+            acc = accp.tile([P, CHUNK], F32, name="acc", tag="acc")
+            acc_of[b] = acc
             for g in range(PASSES):
                 unit = j * PASSES + g
                 nc.tensor.matmul_mx(
@@ -190,76 +239,125 @@ def tile_naswinattention_pa_kernel(
                     stop=(g == PASSES - 1),
                 )
 
-        def e1(c, m):
+        def e1(b):
+            c = b // 8
             y = yp.tile([P, CHUNK], F32, name="y", tag="y")
-            y_of[(c, m)] = y
+            y_of[b] = y
             nc.vector.tensor_tensor(
-                out=y[:], in0=acc_of[(c, m)][:],
+                out=y[:], in0=acc_of[b][:],
                 in1=bias_bc[:, c * CHUNK : (c + 1) * CHUNK], op=ALU.add,
             )
 
-        def e2(c, m):
-            y = y_of[(c, m)]
-            ss = statp.tile([P, 4], F32, name="ss", tag="ss")
-            for h in range(4):
+        def e2(b, heads):
+            y = y_of[b]
+            if b not in ss_of:
+                ss_of[b] = statp.tile([P, 4], F32, name="ss", tag="ss")
+            for h in heads:
                 junk = junkp.tile([P, HD], BF16, name="junk", tag="junk")
                 nc.scalar.activation(
                     out=junk[:], in_=y[:, h * HD : (h + 1) * HD], func=ACT.Square,
-                    accum_out=ss[:, h : h + 1],
+                    accum_out=ss_of[b][:, h : h + 1],
                 )
-            rt = statp.tile([P, 4], F32, name="rt", tag="rt")
-            rt_of[(c, m)] = rt
+
+        def rs(b):
+            r = statp.tile([P, 4], F32, name="rs", tag="rs")
+            rs_of[b] = r
             nc.scalar.activation(
-                out=rt[:], in_=ss[:], func=ACT.Sqrt, bias=eps_t[:], scale=1.0 / HD
+                out=r[:], in_=ss_of[b][:], func=rfunc, bias=eps_t[:], scale=1.0 / HD
             )
 
-        def e3(c, m):
-            y = y_of[(c, m)]
-            rstd = statp.tile([P, 4], F32, name="rstd", tag="rstd")
-            nc.vector.reciprocal(out=rstd[:], in_=rt_of[(c, m)][:])
+        def e3(b):
+            y = y_of[b]
+            gain = g_ps[:, b // 16, :] if GAIN_PSUM else g_bc[:, b // 16, :]
             for h in range(4):
                 hs = slice(h * HD, (h + 1) * HD)
                 nc.vector.scalar_tensor_tensor(
-                    out=y[:, hs], in0=y[:, hs], scalar=rstd[:, h : h + 1],
-                    in1=gains[c // 2][:], op0=ALU.mult, op1=ALU.mult,
+                    out=y[:, hs], in0=y[:, hs], scalar=rs_of[b][:, h : h + 1],
+                    in1=gain, op0=ALU.mult, op1=ALU.mult,
                 )
 
-        def store(c, m):
+        def store(b):
+            c, m = b // 8, b % 8
             j, n = m // 2, m % 2
             half = c % 2
             view = outs[c // 2].rearrange("n (j c) h d -> n j c (h d)", c=P)
             nc.sync.dma_start(
-                out=view[n, j, :, half * CHUNK : (half + 1) * CHUNK], in_=y_of[(c, m)][:]
+                out=view[n, j, :, half * CHUNK : (half + 1) * CHUNK], in_=y_of[b][:]
             )
 
-        for it in prep_items(0):
-            it()
-        for j in range(4):
-            for g in range(PASSES):
-                vid_unit(j, g)
-            mm(0, 2 * j)
-            mm(0, 2 * j + 1)
+        widen_at = {}
+        inter_at = {}
+        quant_at = {}
+        for x in range(3, NUNIT):
+            due = ((x - 2) * 8) // 3 + DUE_SHIFT
+            ioff = IOFF[INTER.get(x, INTER_DEFAULT)]
+            quant_at.setdefault(due, []).append(x)
+            inter_at.setdefault(due - ioff, []).append(x)
+            widen_at.setdefault(due - ioff - 2, []).extend([(x, 0), (x, 1)])
+            widen_at.setdefault(due - ioff - 1, []).extend([(x, 2), (x, 3)])
+        first_tick = min(widen_at)
 
-        for c in range(NCHUNK):
-            items = prep_items(c + 1) if c + 1 < NCHUNK else []
-            normed = c // 2 < 2
-            pos = 0
-            for m in range(8):
-                e1(c, m)
-                if normed:
-                    e2(c, m)
-                else:
-                    store(c, m)
-                upto = min(len(items), ((m + 1) * len(items) + 7) // 8)
-                while pos < upto:
-                    items[pos]()
-                    pos += 1
-                if normed and m >= 1:
-                    e3(c, m - 1)
-                    store(c, m - 1)
-            if normed:
-                e3(c, 7)
-                store(c, 7)
-            if c + 1 < NCHUNK:
-                for m in range(8):
-                    mm(c + 1, m)
+        for t in range(4):
+            widen(0, t)
+        for t in range(4):
+            widen(1, t)
+        for t in range(4):
+            widen(2, t)
+        for g in range(PASSES):
+            vid_t(0, g)
+        interleave(1)
+        interleave(0)
+        quant_w(1)
+        interleave(2)
+        quant_w(0)
+        for g in range(PASSES):
+            vid_x(0, g)
+        for g in range(PASSES):
+            vid_t(1, g)
+        for g in range(PASSES):
+            vid_q(0, g)
+        quant_w(2)
+        for g in range(PASSES):
+            vid_x(1, g)
+        mm(0)
+        mm(1)
+        for g in range(PASSES):
+            vid_q(1, g)
+        mm(2)
+        if GAIN_PSUM:
+            gains_to_psum()
+
+        for b in range(first_tick, NB + E3_LAG + 1):
+            if 0 <= b < NB:
+                e1(b)
+            for j in (2, 3):
+                if b == 2 * j - LEAD:
+                    for g in range(PASSES):
+                        vid_q(j, g)
+            for x in quant_at.get(b, []):
+                quant_w(x)
+            for j in (2, 3):
+                if b == 2 * j - LEAD - 1:
+                    for g in range(PASSES):
+                        vid_t(j, g)
+            if LEAD <= b + LEAD < NB:
+                mm(b + LEAD)
+            if normed(b - 1):
+                e2(b - 1, (0, 1))
+            if normed(b - 2):
+                rs(b - 2)
+            if normed(b - 1):
+                e2(b - 1, (2, 3))
+            for j in (2, 3):
+                if b == 2 * j - LEAD - 1:
+                    for g in range(PASSES):
+                        vid_x(j, g)
+            for x, t in widen_at.get(b, []):
+                widen(x, t)
+            for x in inter_at.get(b, []):
+                interleave(x)
+            if normed(b - E3_LAG):
+                e3(b - E3_LAG)
+                store(b - E3_LAG)
+            if 32 <= b - 1 < NB:
+                store(b - 1)

@@ -20,21 +20,10 @@ NCHUNK = 6
 HD = 128
 EPS = 1e-6
 FLOPS = 2 * TOKENS * K * N
-NB = 48
-NUNIT = 18
 
-LEAD = 3
-E3_LAG = 3
-USE_G = False
-GAIN_PSUM = False
-RSQRT_ON_S = True
-INTER = {}
-INTER_DEFAULT = "V"
-WIDEN_V = {(1, 0), (1, 1), (1, 2), (1, 3)}
-EVAC_V = set()
-DUE_SHIFT = -4
-FAST_INTER = False
-IOFF = {"V": 1, "S": 3, "G": 3}
+WIDEN_ON_V = {(0, 1, 0), (0, 1, 1), (0, 1, 2), (0, 1, 3)}
+G_FROM = 1
+EVAC_ON_S_G = (2,)
 
 
 def tile_naswinattention_pa_kernel(
@@ -47,14 +36,12 @@ def tile_naswinattention_pa_kernel(
         widep = ctx.enter_context(tc.tile_pool(name="widep", bufs=4))
         grpp = ctx.enter_context(tc.tile_pool(name="grpp", bufs=3))
         grpg = ctx.enter_context(tc.tile_pool(name="grpg", bufs=1))
-        vgp = ctx.enter_context(tc.tile_pool(name="vgp", bufs=6))
+        vgp = ctx.enter_context(tc.tile_pool(name="vgp", bufs=4))
         yp = ctx.enter_context(tc.tile_pool(name="yp", bufs=12))
         statp = ctx.enter_context(tc.tile_pool(name="statp", bufs=8))
         junkp = ctx.enter_context(tc.tile_pool(name="junkp", bufs=2))
-        xtp = ctx.enter_context(tc.psum_pool(name="xtp", bufs=3))
-        accp = ctx.enter_context(tc.psum_pool(name="accp", bufs=4 if GAIN_PSUM else 5))
+        psum = ctx.enter_context(tc.psum_pool(name="psum", bufs=7))
         gpp = ctx.enter_context(tc.psum_pool(name="gpp", bufs=1))
-        ctx.enter_context(tc.manual_schedule())
 
         wsc = keep.tile([P, PASSES, 4], F32, name="wsc")
         wbytes = keep.tile([P, PASSES, NCHUNK, 4, CHUNK], U8, name="wbytes")
@@ -64,6 +51,8 @@ def tile_naswinattention_pa_kernel(
         vscl = keep.tile([P, 12, 2, P], U8, name="vscl", align_bytes=64)
         bias_bc = keep.tile([P, N], BF16, name="bias_bc")
         g_bc = keep.tile([P, 2, HD], BF16, name="g_bc")
+        ident_bf = keep.tile([P, P], BF16, name="ident_bf")
+        g_ps = gpp.tile([P, 2, HD], F32, name="g_ps")
         ident = keep.tile([P, P], F32, name="ident")
         perm = keep.tile([P, P], F32, name="perm")
         eps_t = keep.tile([P, 1], F32, name="eps_t")
@@ -88,55 +77,44 @@ def tile_naswinattention_pa_kernel(
             out=wsc[:], in_=w_scale.rearrange("(g p t) o -> p g (t o)", p=P, t=4)
         )
         load_w(0, 0)
+        load_vid(0)
+        load_vid(1)
         load_w(0, 1)
         load_w(0, 2)
-        for a in range(4):
+        for a in range(2, 8):
             load_vid(a)
-        load_w(1, 0)
+        for g in range(PASSES):
+            load_w(1, g)
         nc.sync.dma_start(out=bias_bc[:], in_=bias.partition_broadcast(P))
         nc.sync.dma_start(out=g_bc[:, 0, :], in_=q_gain.partition_broadcast(P))
         nc.sync.dma_start(out=g_bc[:, 1, :], in_=k_gain.partition_broadcast(P))
-        load_vid(4)
-        load_vid(5)
-        load_w(1, 1)
-        load_vid(6)
-        load_vid(7)
-        load_w(1, 2)
         for c in range(2, NCHUNK):
             for g in range(PASSES):
                 load_w(c, g)
 
         nc.vector.memset(eps_t[:], EPS)
-        rfunc = ACT.Abs_reciprocal_sqrt if RSQRT_ON_S else ACT.Sqrt
-        nc.scalar.activation(out=warm[:], in_=eps_t[:], func=rfunc)
+        nc.scalar.activation(out=warm[:], in_=eps_t[:], func=ACT.Abs_reciprocal_sqrt)
         make_identity(nc, ident[:])
         nc.vector.tensor_copy(
             out=perm[:].rearrange("p (n h w) -> p n h w", n=2, h=8, w=8),
             in_=ident[:].rearrange("p (h n w) -> p n h w", h=8, n=2, w=8),
         )
 
-        g_ps = None
-        if GAIN_PSUM:
-            ident_bf = keep.tile([P, P], BF16, name="ident_bf")
-            nc.vector.tensor_copy(out=ident_bf[:], in_=ident[:])
-            g_ps = gpp.tile([P, 2, HD], F32, name="g_ps")
-
-        def gains_to_psum():
-            nc.tensor.matmul(
-                out=g_ps[:].rearrange("p a d -> p (a d)"), lhsT=ident_bf[:],
-                rhs=g_bc[:].rearrange("p a d -> p (a d)"), start=True, stop=True,
-            )
+        nc.vector.tensor_copy(out=ident_bf[:], in_=ident[:])
+        nc.tensor.matmul(
+            out=g_ps[:].rearrange("p a d -> p (a d)"), lhsT=ident_bf[:],
+            rhs=g_bc[:].rearrange("p a d -> p (a d)"), start=True, stop=True,
+        )
 
         wide_of = {}
         grp_of = {}
 
-        def widen(x, t):
-            c, g = x // PASSES, x % PASSES
-            if x not in wide_of:
-                wide_of[x] = widep.tile([P, 4, CHUNK], BF16, name="wide", tag="wide")
-            wide = wide_of[x]
+        def widen(c, g, t):
+            if t == 0:
+                wide_of[(c, g)] = widep.tile([P, 4, CHUNK], BF16, name="wide", tag="wide")
+            wide = wide_of[(c, g)]
             src = wbytes[:, g, c, t, :].bitcast(FP8)
-            if (x, t) in WIDEN_V:
+            if (c, g, t) in WIDEN_ON_V:
                 nc.vector.tensor_scalar(
                     out=wide[:, t, :], in0=src, scalar1=wsc[:, g, t : t + 1],
                     scalar2=None, op0=ALU.mult,
@@ -146,43 +124,38 @@ def tile_naswinattention_pa_kernel(
                     out=wide[:, t, :], in_=src, func=ACT.Copy, scale=wsc[:, g, t : t + 1]
                 )
 
-        def interleave(x):
-            eng = INTER.get(x, INTER_DEFAULT)
-            if eng == "G":
+        def interleave(c, g):
+            src = wide_of[(c, g)][:].rearrange("p t n -> p n t")
+            if c >= G_FROM:
                 grp = grpg.tile([P, CHUNK, 4], BF16, name="grpg", tag="grpg", align_bytes=64)
-            else:
-                grp = grpp.tile([P, CHUNK, 4], BF16, name="grp", tag="grp", align_bytes=64)
-            grp_of[x] = grp
-            if FAST_INTER:
-                dst = grp[:].rearrange("p (c i) t -> p c t i", i=4)
-                src = wide_of[x][:].rearrange("p t (c i) -> p c t i", i=4)
-            else:
-                dst = grp[:]
-                src = wide_of[x][:].rearrange("p t n -> p n t")
-            if eng == "S":
-                nc.scalar.copy(out=dst, in_=src)
-            elif eng == "G":
                 nc.gpsimd.tensor_scalar(
-                    out=dst, in0=src, scalar1=1.0, scalar2=0.0, op0=ALU.mult, op1=ALU.add
+                    out=grp[:], in0=src, scalar1=1.0, scalar2=0.0, op0=ALU.mult, op1=ALU.add
                 )
             else:
-                nc.vector.tensor_copy(out=dst, in_=src)
+                grp = grpp.tile([P, CHUNK, 4], BF16, name="grp", tag="grp", align_bytes=64)
+                nc.vector.tensor_copy(out=grp[:], in_=src)
+            grp_of[(c, g)] = grp
 
-        def quant_w(x):
-            c, g = x // PASSES, x % PASSES
+        def quant_w(c, g):
             cols = slice(c * CHUNK, (c + 1) * CHUNK)
             nc.vector.quantize_mx(
                 out=wcodes[:, g, cols].bitcast(FP8X4),
                 scales=wscl[:, g, cols],
-                in_=grp_of[x][:].rearrange("p n t -> p (n t)"),
+                in_=grp_of[(c, g)][:].rearrange("p n t -> p (n t)"),
             )
 
-        xt_of = {}
-        vg_of = {}
+        def prep_items(c):
+            items = []
+            for g in range(PASSES):
+                for t in range(4):
+                    items.append(lambda c=c, g=g, t=t: widen(c, g, t))
+                items.append(lambda c=c, g=g: interleave(c, g))
+                items.append(lambda c=c, g=g: quant_w(c, g))
+            return items
 
-        def vid_t(j, g):
-            xt = xtp.tile([P, 2, 2, P], F32, name="xt", tag="xt")
-            xt_of[(j, g)] = xt
+        def vid_unit(j, g):
+            unit = j * PASSES + g
+            xt = psum.tile([P, 2, 2, P], F32, name="xt", tag="bank")
             for a2 in range(2):
                 words = vraw[2 * j + a2][:].bitcast(F32)
                 for u in range(2):
@@ -191,42 +164,31 @@ def tile_naswinattention_pa_kernel(
                         words[:, 256 * g + u : 256 * (g + 1) : 2],
                         perm[:],
                     )
-
-        def vid_x(j, g):
-            xt = xt_of[(j, g)]
             vg = vgp.tile([P, 2, 256], F32, name="vg", tag="vg", align_bytes=64)
-            vg_of[(j, g)] = vg
             for n in range(2):
                 dst = vg[:, n, :].rearrange("p (a c u) -> p a c u", a=2, c=64, u=2)
                 src = xt[:, :, :, n * 64 : (n + 1) * 64].rearrange("p a u c -> p a c u")
-                if (j, g) in EVAC_V:
-                    nc.vector.tensor_copy(out=dst, in_=src)
-                else:
+                if g in EVAC_ON_S_G:
                     nc.scalar.copy(out=dst, in_=src)
-
-        def vid_q(j, g):
-            unit = j * PASSES + g
+                else:
+                    nc.vector.tensor_copy(out=dst, in_=src)
             nc.vector.quantize_mx(
                 out=vcodes[:, unit, :, :].rearrange("p n c -> p (n c)").bitcast(FP8X4),
                 scales=vscl[:, unit, :, :].rearrange("p n c -> p (n c)"),
-                in_=vg_of[(j, g)][:].rearrange("p n w -> p (n w)").bitcast(BF16),
+                in_=vg[:].rearrange("p n w -> p (n w)").bitcast(BF16),
             )
 
         acc_of = {}
         y_of = {}
         ss_of = {}
-        rs_of = {}
+        rt_of = {}
         outs = (out_q, out_k, out_v)
 
-        def normed(b):
-            return 0 <= b < 32
-
-        def mm(b):
-            c, m = b // 8, b % 8
+        def mm(c, m):
             j, n = m // 2, m % 2
             cols = slice(c * CHUNK, (c + 1) * CHUNK)
-            acc = accp.tile([P, CHUNK], F32, name="acc", tag="acc")
-            acc_of[b] = acc
+            acc = psum.tile([P, CHUNK], F32, name="acc", tag="bank")
+            acc_of[(c, m)] = acc
             for g in range(PASSES):
                 unit = j * PASSES + g
                 nc.tensor.matmul_mx(
@@ -239,125 +201,75 @@ def tile_naswinattention_pa_kernel(
                     stop=(g == PASSES - 1),
                 )
 
-        def e1(b):
-            c = b // 8
+        def e1(c, m):
             y = yp.tile([P, CHUNK], F32, name="y", tag="y")
-            y_of[b] = y
+            y_of[(c, m)] = y
             nc.vector.tensor_tensor(
-                out=y[:], in0=acc_of[b][:],
+                out=y[:], in0=acc_of[(c, m)][:],
                 in1=bias_bc[:, c * CHUNK : (c + 1) * CHUNK], op=ALU.add,
             )
 
-        def e2(b, heads):
-            y = y_of[b]
-            if b not in ss_of:
-                ss_of[b] = statp.tile([P, 4], F32, name="ss", tag="ss")
-            for h in heads:
+        def e2(c, m):
+            y = y_of[(c, m)]
+            ss = statp.tile([P, 4], F32, name="ss", tag="ss")
+            for h in range(4):
                 junk = junkp.tile([P, HD], BF16, name="junk", tag="junk")
                 nc.scalar.activation(
                     out=junk[:], in_=y[:, h * HD : (h + 1) * HD], func=ACT.Square,
-                    accum_out=ss_of[b][:, h : h + 1],
+                    accum_out=ss[:, h : h + 1],
                 )
-
-        def rs(b):
-            r = statp.tile([P, 4], F32, name="rs", tag="rs")
-            rs_of[b] = r
+            rt = statp.tile([P, 4], F32, name="rt", tag="rt")
+            rt_of[(c, m)] = rt
             nc.scalar.activation(
-                out=r[:], in_=ss_of[b][:], func=rfunc, bias=eps_t[:], scale=1.0 / HD
+                out=rt[:], in_=ss[:], func=ACT.Abs_reciprocal_sqrt, bias=eps_t[:], scale=1.0 / HD
             )
 
-        def e3(b):
-            y = y_of[b]
-            gain = g_ps[:, b // 16, :] if GAIN_PSUM else g_bc[:, b // 16, :]
+        def e3(c, m):
+            y = y_of[(c, m)]
+            rstd = rt_of[(c, m)]
             for h in range(4):
                 hs = slice(h * HD, (h + 1) * HD)
                 nc.vector.scalar_tensor_tensor(
-                    out=y[:, hs], in0=y[:, hs], scalar=rs_of[b][:, h : h + 1],
-                    in1=gain, op0=ALU.mult, op1=ALU.mult,
+                    out=y[:, hs], in0=y[:, hs], scalar=rstd[:, h : h + 1],
+                    in1=g_ps[:, c // 2, :], op0=ALU.mult, op1=ALU.mult,
                 )
 
-        def store(b):
-            c, m = b // 8, b % 8
+        def store(c, m):
             j, n = m // 2, m % 2
             half = c % 2
             view = outs[c // 2].rearrange("n (j c) h d -> n j c (h d)", c=P)
             nc.sync.dma_start(
-                out=view[n, j, :, half * CHUNK : (half + 1) * CHUNK], in_=y_of[b][:]
+                out=view[n, j, :, half * CHUNK : (half + 1) * CHUNK], in_=y_of[(c, m)][:]
             )
 
-        widen_at = {}
-        inter_at = {}
-        quant_at = {}
-        for x in range(3, NUNIT):
-            due = ((x - 2) * 8) // 3 + DUE_SHIFT
-            ioff = IOFF[INTER.get(x, INTER_DEFAULT)]
-            quant_at.setdefault(due, []).append(x)
-            inter_at.setdefault(due - ioff, []).append(x)
-            widen_at.setdefault(due - ioff - 2, []).extend([(x, 0), (x, 1)])
-            widen_at.setdefault(due - ioff - 1, []).extend([(x, 2), (x, 3)])
-        first_tick = min(widen_at)
+        for it in prep_items(0):
+            it()
+        for j in range(4):
+            for g in range(PASSES):
+                vid_unit(j, g)
+            mm(0, 2 * j)
+            mm(0, 2 * j + 1)
 
-        for t in range(4):
-            widen(0, t)
-        for t in range(4):
-            widen(1, t)
-        for t in range(4):
-            widen(2, t)
-        for g in range(PASSES):
-            vid_t(0, g)
-        interleave(1)
-        interleave(0)
-        quant_w(1)
-        interleave(2)
-        quant_w(0)
-        for g in range(PASSES):
-            vid_x(0, g)
-        for g in range(PASSES):
-            vid_t(1, g)
-        for g in range(PASSES):
-            vid_q(0, g)
-        quant_w(2)
-        for g in range(PASSES):
-            vid_x(1, g)
-        mm(0)
-        mm(1)
-        for g in range(PASSES):
-            vid_q(1, g)
-        mm(2)
-        if GAIN_PSUM:
-            gains_to_psum()
-
-        for b in range(first_tick, NB + E3_LAG + 1):
-            if 0 <= b < NB:
-                e1(b)
-            for j in (2, 3):
-                if b == 2 * j - LEAD:
-                    for g in range(PASSES):
-                        vid_q(j, g)
-            for x in quant_at.get(b, []):
-                quant_w(x)
-            for j in (2, 3):
-                if b == 2 * j - LEAD - 1:
-                    for g in range(PASSES):
-                        vid_t(j, g)
-            if LEAD <= b + LEAD < NB:
-                mm(b + LEAD)
-            if normed(b - 1):
-                e2(b - 1, (0, 1))
-            if normed(b - 2):
-                rs(b - 2)
-            if normed(b - 1):
-                e2(b - 1, (2, 3))
-            for j in (2, 3):
-                if b == 2 * j - LEAD - 1:
-                    for g in range(PASSES):
-                        vid_x(j, g)
-            for x, t in widen_at.get(b, []):
-                widen(x, t)
-            for x in inter_at.get(b, []):
-                interleave(x)
-            if normed(b - E3_LAG):
-                e3(b - E3_LAG)
-                store(b - E3_LAG)
-            if 32 <= b - 1 < NB:
-                store(b - 1)
+        for c in range(NCHUNK):
+            items = prep_items(c + 1) if c + 1 < NCHUNK else []
+            normed = c // 2 < 2
+            pos = 0
+            for m in range(8):
+                e1(c, m)
+                if normed:
+                    e2(c, m)
+                else:
+                    store(c, m)
+                upto = min(len(items), ((m + 1) * len(items) + 7) // 8)
+                while pos < upto:
+                    items[pos]()
+                    pos += 1
+                if normed and m >= 1:
+                    e3(c, m - 1)
+                    store(c, m - 1)
+            if normed:
+                e3(c, 7)
+                store(c, 7)
+            if c + 1 < NCHUNK:
+                for m in range(8):
+                    mm(c + 1, m)

@@ -81,10 +81,12 @@ def tile_naswinattention_pa_kernel(
         load_vid(1)
         load_w(0, 1)
         load_w(0, 2)
-        for a in range(2, 8):
-            load_vid(a)
+        load_vid(2)
+        load_vid(3)
         for g in range(PASSES):
             load_w(1, g)
+        for a in range(4, 8):
+            load_vid(a)
         nc.sync.dma_start(out=bias_bc[:], in_=bias.partition_broadcast(P))
         nc.sync.dma_start(out=g_bc[:, 0, :], in_=q_gain.partition_broadcast(P))
         nc.sync.dma_start(out=g_bc[:, 1, :], in_=k_gain.partition_broadcast(P))
@@ -153,9 +155,12 @@ def tile_naswinattention_pa_kernel(
                 items.append(lambda c=c, g=g: quant_w(c, g))
             return items
 
-        def vid_unit(j, g):
-            unit = j * PASSES + g
+        xt_of = {}
+        vg_of = {}
+
+        def vid_turn(j, g):
             xt = psum.tile([P, 2, 2, P], F32, name="xt", tag="bank")
+            xt_of[(j, g)] = xt
             for a2 in range(2):
                 words = vraw[2 * j + a2][:].bitcast(F32)
                 for u in range(2):
@@ -164,7 +169,11 @@ def tile_naswinattention_pa_kernel(
                         words[:, 256 * g + u : 256 * (g + 1) : 2],
                         perm[:],
                     )
+
+        def vid_out(j, g):
+            xt = xt_of[(j, g)]
             vg = vgp.tile([P, 2, 256], F32, name="vg", tag="vg", align_bytes=64)
+            vg_of[(j, g)] = vg
             for n in range(2):
                 dst = vg[:, n, :].rearrange("p (a c u) -> p a c u", a=2, c=64, u=2)
                 src = xt[:, :, :, n * 64 : (n + 1) * 64].rearrange("p a u c -> p a c u")
@@ -172,6 +181,10 @@ def tile_naswinattention_pa_kernel(
                     nc.scalar.copy(out=dst, in_=src)
                 else:
                     nc.vector.tensor_copy(out=dst, in_=src)
+
+        def vid_quant(j, g):
+            unit = j * PASSES + g
+            vg = vg_of[(j, g)]
             nc.vector.quantize_mx(
                 out=vcodes[:, unit, :, :].rearrange("p n c -> p (n c)").bitcast(FP8X4),
                 scales=vscl[:, unit, :, :].rearrange("p n c -> p (n c)"),
@@ -242,13 +255,25 @@ def tile_naswinattention_pa_kernel(
                 out=view[n, j, :, half * CHUNK : (half + 1) * CHUNK], in_=y_of[(c, m)][:]
             )
 
-        for it in prep_items(0):
-            it()
-        for j in range(4):
-            for g in range(PASSES):
-                vid_unit(j, g)
-            mm(0, 2 * j)
-            mm(0, 2 * j + 1)
+        for g in range(PASSES):
+            for t in range(4):
+                widen(0, g, t)
+            interleave(0, g)
+            if g >= 1:
+                quant_w(0, g - 1)
+        units = [(j, g) for j in range(4) for g in range(PASSES)]
+        vid_turn(*units[0])
+        vid_out(*units[0])
+        quant_w(0, PASSES - 1)
+        for i in range(1, len(units) + 1):
+            if i < len(units):
+                vid_turn(*units[i])
+                vid_out(*units[i])
+            j, g = units[i - 1]
+            vid_quant(j, g)
+            if g == PASSES - 1:
+                mm(0, 2 * j)
+                mm(0, 2 * j + 1)
 
         for c in range(NCHUNK):
             items = prep_items(c + 1) if c + 1 < NCHUNK else []

@@ -24,6 +24,7 @@ FLOPS = 2 * TOKENS * K * N
 WIDEN_ON_V = {(0, 1, 0), (0, 1, 1), (0, 1, 2), (0, 1, 3)}
 G_FROM = 1
 EVAC_ON_S_G = (2,)
+LAG = 3
 
 
 def tile_naswinattention_pa_kernel(
@@ -289,12 +290,10 @@ def tile_naswinattention_pa_kernel(
                 while pos < upto:
                     items[pos]()
                     pos += 1
-                if normed and m >= 1:
-                    e3(c, m - 1)
-                    store(c, m - 1)
-            if normed:
-                e3(c, 7)
-                store(c, 7)
+                late = 8 * c + m - LAG
+                if 0 <= late < 32:
+                    e3(late // 8, late % 8)
+                    store(late // 8, late % 8)
             if c + 1 < NCHUNK:
                 for m in range(8):
                     mm(c + 1, m)

@@ -21,9 +21,11 @@ HD = 128
 EPS = 1e-6
 FLOPS = 2 * TOKENS * K * N
 
-WIDEN_ON_V = {(0, 1, 0), (0, 1, 1), (0, 1, 2), (0, 1, 3)}
+WIDEN_ON_V = {(0, g, t) for g in (0, 1) for t in range(4)}
 G_FROM = 1
-EVAC_ON_S_G = (2,)
+EVAC_ON_S_G = (1, 2)
+ORDER = (0, 1, 2, 4, 3, 5)
+NORMED = 4
 LAG = 3
 
 
@@ -78,10 +80,10 @@ def tile_naswinattention_pa_kernel(
             out=wsc[:], in_=w_scale.rearrange("(g p t) o -> p g (t o)", p=P, t=4)
         )
         load_w(0, 0)
-        load_vid(0)
-        load_vid(1)
         load_w(0, 1)
         load_w(0, 2)
+        load_vid(0)
+        load_vid(1)
         load_vid(2)
         load_vid(3)
         for g in range(PASSES):
@@ -91,7 +93,7 @@ def tile_naswinattention_pa_kernel(
         nc.sync.dma_start(out=bias_bc[:], in_=bias.partition_broadcast(P))
         nc.sync.dma_start(out=g_bc[:, 0, :], in_=q_gain.partition_broadcast(P))
         nc.sync.dma_start(out=g_bc[:, 1, :], in_=k_gain.partition_broadcast(P))
-        for c in range(2, NCHUNK):
+        for c in ORDER[2:]:
             for g in range(PASSES):
                 load_w(c, g)
 
@@ -276,13 +278,14 @@ def tile_naswinattention_pa_kernel(
                 mm(0, 2 * j)
                 mm(0, 2 * j + 1)
 
-        for c in range(NCHUNK):
-            items = prep_items(c + 1) if c + 1 < NCHUNK else []
-            normed = c // 2 < 2
+        banks = [(c, m) for c in ORDER for m in range(8)]
+        for i in range(NCHUNK):
+            c = ORDER[i]
+            items = prep_items(ORDER[i + 1]) if i + 1 < NCHUNK else []
             pos = 0
             for m in range(8):
                 e1(c, m)
-                if normed:
+                if c < NORMED:
                     e2(c, m)
                 else:
                     store(c, m)
@@ -290,10 +293,13 @@ def tile_naswinattention_pa_kernel(
                 while pos < upto:
                     items[pos]()
                     pos += 1
-                late = 8 * c + m - LAG
-                if 0 <= late < 32:
-                    e3(late // 8, late % 8)
-                    store(late // 8, late % 8)
-            if c + 1 < NCHUNK:
+                if 8 * i + m >= LAG and banks[8 * i + m - LAG][0] < NORMED:
+                    e3(*banks[8 * i + m - LAG])
+                    store(*banks[8 * i + m - LAG])
+            if i + 1 < NCHUNK:
                 for m in range(8):
-                    mm(c + 1, m)
+                    mm(ORDER[i + 1], m)
+        for bank in banks[len(banks) - LAG :]:
+            if bank[0] < NORMED:
+                e3(*bank)
+                store(*bank)

@@ -221,8 +221,8 @@ def tile_naswinattention_pa_kernel(
             y = yp.tile([P, CHUNK], F32, name="y", tag="y")
             y_of[(c, m)] = y
             nc.vector.tensor_tensor(
-                out=y[:], in0=acc_of[(c, m)][:],
-                in1=bias_bc[:, c * CHUNK : (c + 1) * CHUNK], op=ALU.add,
+                out=y[:], in0=bias_bc[:, c * CHUNK : (c + 1) * CHUNK],
+                in1=acc_of[(c, m)][:], op=ALU.add,
             )
 
         def e2(c, m):

@@ -22,7 +22,7 @@ EPS = 1e-6
 FLOPS = 2 * TOKENS * K * N
 
 WIDEN_ON_V = {(0, g, t) for g in (0, 1) for t in range(4)}
-G_FROM = 1
+G_FROM = 2
 EVAC_ON_S_G = (1, 2)
 ORDER = (0, 1, 2, 4, 3, 5)
 NORMED = 4

@@ -36,7 +36,7 @@ def tile_naswinattention_pa_kernel(
     with ExitStack() as ctx:
         keep = ctx.enter_context(tc.tile_pool(name="keep", bufs=1))
         vrawp = ctx.enter_context(tc.tile_pool(name="vrawp", bufs=8))
-        widep = ctx.enter_context(tc.tile_pool(name="widep", bufs=4))
+        widep = ctx.enter_context(tc.tile_pool(name="widep", bufs=8))
         grpp = ctx.enter_context(tc.tile_pool(name="grpp", bufs=3))
         grpg = ctx.enter_context(tc.tile_pool(name="grpg", bufs=1))
         vgp = ctx.enter_context(tc.tile_pool(name="vgp", bufs=4))

@@ -21,7 +21,7 @@ HD = 128
 EPS = 1e-6
 FLOPS = 2 * TOKENS * K * N
 
-WIDEN_ON_V = {(0, g, t) for g in (0, 1) for t in range(4)}
+WIDEN_ON_V = {(0, g, t) for g in (0, 1) for t in range(2)}
 G_FROM = 2
 EVAC_ON_S_G = (1, 2)
 ORDER = (0, 1, 2, 4, 3, 5)
@@ -47,7 +47,7 @@ def tile_naswinattention_pa_kernel(
         gpp = ctx.enter_context(tc.psum_pool(name="gpp", bufs=1))
 
         wsc = keep.tile([P, PASSES, 4], F32, name="wsc")
-        wbytes = keep.tile([P, PASSES, NCHUNK, 4, CHUNK], U8, name="wbytes")
+        wbytes = keep.tile([P, PASSES, NCHUNK // 2, 4, 2 * CHUNK], U8, name="wbytes")
         wcodes = keep.tile([P, PASSES, N], U32, name="wcodes", align_bytes=64)
         wscl = keep.tile([P, PASSES, N], U8, name="wscl", align_bytes=64)
         vcodes = keep.tile([P, 12, 2, P], U32, name="vcodes", align_bytes=64)
@@ -63,10 +63,10 @@ def tile_naswinattention_pa_kernel(
 
         w_view = w_bytes.rearrange("(g p t) n -> g p t n", p=P, t=4)
 
-        def load_w(c, g):
+        def load_w(pair, g, t0=0, t1=4):
             nc.sync.dma_start(
-                out=wbytes[:, g, c, :, :],
-                in_=w_view[g, :, :, c * CHUNK : (c + 1) * CHUNK],
+                out=wbytes[:, g, pair, t0:t1, :],
+                in_=w_view[g, :, t0:t1, pair * 2 * CHUNK : (pair + 1) * 2 * CHUNK],
             )
 
         vraw = []
@@ -79,23 +79,18 @@ def tile_naswinattention_pa_kernel(
         nc.sync.dma_start(
             out=wsc[:], in_=w_scale.rearrange("(g p t) o -> p g (t o)", p=P, t=4)
         )
-        load_w(0, 0)
+        load_w(0, 0, 0, 2)
+        load_w(0, 0, 2, 4)
         load_w(0, 1)
         load_w(0, 2)
-        load_vid(0)
-        load_vid(1)
-        load_vid(2)
-        load_vid(3)
-        for g in range(PASSES):
-            load_w(1, g)
-        for a in range(4, 8):
+        for a in range(8):
             load_vid(a)
         nc.sync.dma_start(out=bias_bc[:], in_=bias.partition_broadcast(P))
         nc.sync.dma_start(out=g_bc[:, 0, :], in_=q_gain.partition_broadcast(P))
         nc.sync.dma_start(out=g_bc[:, 1, :], in_=k_gain.partition_broadcast(P))
-        for c in ORDER[2:]:
+        for pair in (1, 2):
             for g in range(PASSES):
-                load_w(c, g)
+                load_w(pair, g)
 
         nc.vector.memset(eps_t[:], EPS)
         nc.scalar.activation(out=warm[:], in_=eps_t[:], func=ACT.Abs_reciprocal_sqrt)
@@ -118,7 +113,8 @@ def tile_naswinattention_pa_kernel(
             if t == 0:
                 wide_of[(c, g)] = widep.tile([P, 4, CHUNK], BF16, name="wide", tag="wide")
             wide = wide_of[(c, g)]
-            src = wbytes[:, g, c, t, :].bitcast(FP8)
+            half = c % 2
+            src = wbytes[:, g, c // 2, t, half * CHUNK : (half + 1) * CHUNK].bitcast(FP8)
             if (c, g, t) in WIDEN_ON_V:
                 nc.vector.tensor_scalar(
                     out=wide[:, t, :], in0=src, scalar1=wsc[:, g, t : t + 1],

@@ -21,12 +21,151 @@ HD = 128
 EPS = 1e-6
 FLOPS = 2 * TOKENS * K * N
 
-WIDEN_ON_V = {(0, g, t) for g in (0, 1) for t in range(2)}
-G_FROM = 2
-EVAC_ON_S_G = (1, 2)
+WIDEN_ON_V = {(0, g, t) for g in (0, 1) for t in (0, 1)}
+G_FROM = 1
+OUT_ON_S = (1, 2)
 ORDER = (0, 1, 2, 4, 3, 5)
 NORMED = 4
-LAG = 3
+LAG = 6
+QUANT_EVERY = 5
+QUANT_FROM = 2
+AHEAD = 7
+SETTLE = 3
+HEAD_PLANES = (3, 6, 9, 12)
+
+
+def make_plan():
+    plan = []
+    banks = TOKENS // P * NCHUNK
+    normed = [b for b in range(banks) if ORDER[b // 8] < NORMED]
+    planes = [(i, g, t) for i in range(1, NCHUNK) for g in range(PASSES) for t in range(4)]
+    units = [(i, g) for i in range(1, NCHUNK) for g in range(PASSES)]
+    at = {"plane": 0, "lay": 0, "quant": 0, "open": 0, "add": 0, "scale": 0, "pass": 0, "since": SETTLE}
+    vid_parts = set()
+    quantized = {(0, g) for g in range(PASSES)}
+    done = {}
+
+    def widen_to(n):
+        while at["plane"] < min(n, len(planes)):
+            plan.append(("widen",) + planes[at["plane"]])
+            at["plane"] += 1
+
+    def lay():
+        while at["lay"] < len(units):
+            u = at["lay"]
+            if 4 * (u + 1) > at["plane"] or (u > 0 and units[u - 1] not in quantized):
+                break
+            plan.append(("lay",) + units[u])
+            at["lay"] += 1
+
+    def multiply():
+        while at["open"] < min(banks, at["add"] + AHEAD):
+            b = at["open"]
+            if (b // 8, 0) not in quantized or (b < 8 and b // 2 not in vid_parts):
+                break
+            done[b] = 0
+            at["open"] += 1
+        for b in range(at["open"]):
+            while done[b] < PASSES and (b // 8, done[b]) in quantized:
+                plan.append(("multiply", b, done[b]))
+                done[b] += 1
+
+    def quantize_next():
+        i, g = units[at["quant"]]
+        widen_to(4 * (at["quant"] + 1))
+        lay()
+        plan.append(("quantize", i, g))
+        quantized.add((i, g))
+        at["quant"] += 1
+        if g == PASSES - 1:
+            at["since"] = 0
+        lay()
+        multiply()
+
+    def epilogue_pass():
+        b = at["add"]
+        waiting = sum(1 for n in normed if n < b) - at["scale"]
+        can_add = b < banks and done.get(b, 0) == PASSES
+        can_scale = waiting > 0 and (normed[at["scale"]] | 1) < b
+        settling = b % 8 == 0 and at["since"] < SETTLE
+        if can_add and not (can_scale and (waiting >= LAG or settling)):
+            plan.append(("add", b))
+            at["add"] += 1
+            if b in normed:
+                plan.append(("square", b))
+            else:
+                plan.append(("store", b))
+            multiply()
+        elif can_scale:
+            plan.append(("scale", normed[at["scale"]]))
+            plan.append(("store", normed[at["scale"]]))
+            at["scale"] += 1
+        else:
+            return False
+        at["pass"] += 1
+        at["since"] += 1
+        return True
+
+    for g in range(PASSES):
+        for t in range(4):
+            plan.append(("widen", 0, g, t))
+    for g in range(PASSES):
+        plan.append(("lay", 0, g))
+        if g > 0:
+            plan.append(("quantize", 0, g - 1))
+    for g in range(PASSES):
+        plan.append(("turn", 0, g))
+    plan.append(("empty", 0, 0))
+    plan.append(("turn", 1, 0))
+    plan.append(("quantize", 0, PASSES - 1))
+    for g in (1, 2):
+        plan.append(("empty", 0, g))
+        plan.append(("turn", 1, g))
+    widen_to(HEAD_PLANES[0])
+    plan.append(("vid_quantize", 0, 0))
+    plan.append(("vid_quantize", 0, 1))
+    plan.append(("empty", 1, 0))
+    plan.append(("turn", 2, 0))
+    plan.append(("vid_quantize", 0, 2))
+    vid_parts.add(0)
+    multiply()
+    for g in (1, 2):
+        plan.append(("empty", 1, g))
+        plan.append(("turn", 2, g))
+    widen_to(HEAD_PLANES[1])
+    for g in range(PASSES):
+        plan.append(("vid_quantize", 1, g))
+    vid_parts.add(1)
+    lay()
+    multiply()
+    for j in (2, 3):
+        for g in range(PASSES):
+            plan.append(("empty", j, g))
+            if j == 2:
+                plan.append(("turn", 3, g))
+        widen_to(HEAD_PLANES[j])
+        epilogue_pass()
+        epilogue_pass()
+        for g in range(PASSES):
+            plan.append(("vid_quantize", j, g))
+        vid_parts.add(j)
+        if j == 2:
+            quantize_next()
+        multiply()
+    plan.append(("gains",))
+
+    at["pass"] = 0
+    first = at["quant"]
+    while at["add"] < banks or at["scale"] < len(normed):
+        while at["quant"] < len(units) and (
+            at["pass"] >= QUANT_FROM + QUANT_EVERY * (at["quant"] - first)
+        ):
+            quantize_next()
+        if not epilogue_pass():
+            quantize_next()
+        widen_to(HEAD_PLANES[-1] + at["pass"])
+        lay()
+    return plan
 
 
 def tile_naswinattention_pa_kernel(
@@ -34,13 +173,14 @@ def tile_naswinattention_pa_kernel(
 ):
     nc = tc.nc
     with ExitStack() as ctx:
+        ctx.enter_context(tc.manual_schedule())
         keep = ctx.enter_context(tc.tile_pool(name="keep", bufs=1))
         vrawp = ctx.enter_context(tc.tile_pool(name="vrawp", bufs=8))
         widep = ctx.enter_context(tc.tile_pool(name="widep", bufs=8))
         grpp = ctx.enter_context(tc.tile_pool(name="grpp", bufs=3))
         grpg = ctx.enter_context(tc.tile_pool(name="grpg", bufs=1))
         vgp = ctx.enter_context(tc.tile_pool(name="vgp", bufs=4))
-        yp = ctx.enter_context(tc.tile_pool(name="yp", bufs=12))
+        yp = ctx.enter_context(tc.tile_pool(name="yp", bufs=18))
         statp = ctx.enter_context(tc.tile_pool(name="statp", bufs=8))
         junkp = ctx.enter_context(tc.tile_pool(name="junkp", bufs=2))
         psum = ctx.enter_context(tc.psum_pool(name="psum", bufs=7))
@@ -99,23 +239,25 @@ def tile_naswinattention_pa_kernel(
             out=perm[:].rearrange("p (n h w) -> p n h w", n=2, h=8, w=8),
             in_=ident[:].rearrange("p (h n w) -> p n h w", h=8, n=2, w=8),
         )
-
         nc.vector.tensor_copy(out=ident_bf[:], in_=ident[:])
-        nc.tensor.matmul(
-            out=g_ps[:].rearrange("p a d -> p (a d)"), lhsT=ident_bf[:],
-            rhs=g_bc[:].rearrange("p a d -> p (a d)"), start=True, stop=True,
-        )
+
+        def spread_gains():
+            nc.tensor.matmul(
+                out=g_ps[:].rearrange("p a d -> p (a d)"), lhsT=ident_bf[:],
+                rhs=g_bc[:].rearrange("p a d -> p (a d)"), start=True, stop=True,
+            )
 
         wide_of = {}
         grp_of = {}
 
-        def widen(c, g, t):
+        def widen(i, g, t):
+            c = ORDER[i]
             if t == 0:
-                wide_of[(c, g)] = widep.tile([P, 4, CHUNK], BF16, name="wide", tag="wide")
-            wide = wide_of[(c, g)]
+                wide_of[(i, g)] = widep.tile([P, 4, CHUNK], BF16, name="wide", tag="wide")
+            wide = wide_of[(i, g)]
             half = c % 2
             src = wbytes[:, g, c // 2, t, half * CHUNK : (half + 1) * CHUNK].bitcast(FP8)
-            if (c, g, t) in WIDEN_ON_V:
+            if (i, g, t) in WIDEN_ON_V:
                 nc.vector.tensor_scalar(
                     out=wide[:, t, :], in0=src, scalar1=wsc[:, g, t : t + 1],
                     scalar2=None, op0=ALU.mult,
@@ -125,9 +267,9 @@ def tile_naswinattention_pa_kernel(
                     out=wide[:, t, :], in_=src, func=ACT.Copy, scale=wsc[:, g, t : t + 1]
                 )
 
-        def interleave(c, g):
-            src = wide_of[(c, g)][:].rearrange("p t n -> p n t")
-            if c >= G_FROM:
+        def lay(i, g):
+            src = wide_of[(i, g)][:].rearrange("p t n -> p n t")
+            if i >= G_FROM:
                 grp = grpg.tile([P, CHUNK, 4], BF16, name="grpg", tag="grpg", align_bytes=64)
                 nc.gpsimd.tensor_scalar(
                     out=grp[:], in0=src, scalar1=1.0, scalar2=0.0, op0=ALU.mult, op1=ALU.add
@@ -135,53 +277,43 @@ def tile_naswinattention_pa_kernel(
             else:
                 grp = grpp.tile([P, CHUNK, 4], BF16, name="grp", tag="grp", align_bytes=64)
                 nc.vector.tensor_copy(out=grp[:], in_=src)
-            grp_of[(c, g)] = grp
+            grp_of[(i, g)] = grp
 
-        def quant_w(c, g):
-            cols = slice(c * CHUNK, (c + 1) * CHUNK)
+        def quantize(i, g):
+            cols = slice(i * CHUNK, (i + 1) * CHUNK)
             nc.vector.quantize_mx(
                 out=wcodes[:, g, cols].bitcast(FP8X4),
                 scales=wscl[:, g, cols],
-                in_=grp_of[(c, g)][:].rearrange("p n t -> p (n t)"),
+                in_=grp_of[(i, g)][:].rearrange("p n t -> p (n t)"),
             )
-
-        def prep_items(c):
-            items = []
-            for g in range(PASSES):
-                for t in range(4):
-                    items.append(lambda c=c, g=g, t=t: widen(c, g, t))
-                items.append(lambda c=c, g=g: interleave(c, g))
-                items.append(lambda c=c, g=g: quant_w(c, g))
-            return items
 
         xt_of = {}
         vg_of = {}
 
-        def vid_turn(j, g):
-            xt = psum.tile([P, 2, 2, P], F32, name="xt", tag="bank")
+        def turn(j, g):
+            xt = psum.tile([P, 2, 2, 2, 64], F32, name="xt", tag="bank")
             xt_of[(j, g)] = xt
             for a2 in range(2):
                 words = vraw[2 * j + a2][:].bitcast(F32)
                 for u in range(2):
                     nc.tensor.transpose(
-                        xt[:, a2, u, :],
+                        xt[:, :, u, a2, :],
                         words[:, 256 * g + u : 256 * (g + 1) : 2],
                         perm[:],
                     )
 
-        def vid_out(j, g):
+        def empty(j, g):
             xt = xt_of[(j, g)]
             vg = vgp.tile([P, 2, 256], F32, name="vg", tag="vg", align_bytes=64)
             vg_of[(j, g)] = vg
-            for n in range(2):
-                dst = vg[:, n, :].rearrange("p (a c u) -> p a c u", a=2, c=64, u=2)
-                src = xt[:, :, :, n * 64 : (n + 1) * 64].rearrange("p a u c -> p a c u")
-                if g in EVAC_ON_S_G:
-                    nc.scalar.copy(out=dst, in_=src)
-                else:
-                    nc.vector.tensor_copy(out=dst, in_=src)
+            dst = vg[:].rearrange("p n (ac u) -> p n ac u", u=2)
+            src = xt[:].rearrange("p n u a c -> p n (a c) u")
+            if g in OUT_ON_S:
+                nc.scalar.copy(out=dst, in_=src)
+            else:
+                nc.vector.tensor_copy(out=dst, in_=src)
 
-        def vid_quant(j, g):
+        def vid_quantize(j, g):
             unit = j * PASSES + g
             vg = vg_of[(j, g)]
             nc.vector.quantize_mx(
@@ -196,106 +328,72 @@ def tile_naswinattention_pa_kernel(
         rt_of = {}
         outs = (out_q, out_k, out_v)
 
-        def mm(c, m):
-            j, n = m // 2, m % 2
-            cols = slice(c * CHUNK, (c + 1) * CHUNK)
-            acc = psum.tile([P, CHUNK], F32, name="acc", tag="bank")
-            acc_of[(c, m)] = acc
-            for g in range(PASSES):
-                unit = j * PASSES + g
-                nc.tensor.matmul_mx(
-                    out=acc[:],
-                    lhsT=vcodes[:, unit, n, :].bitcast(FP8X4),
-                    lhsT_scale=vscl[:, unit, n, :],
-                    rhs=wcodes[:, g, cols].bitcast(FP8X4),
-                    rhs_scale=wscl[:, g, cols],
-                    start=(g == 0),
-                    stop=(g == PASSES - 1),
-                )
-
-        def e1(c, m):
-            y = yp.tile([P, CHUNK], F32, name="y", tag="y")
-            y_of[(c, m)] = y
-            nc.vector.tensor_tensor(
-                out=y[:], in0=bias_bc[:, c * CHUNK : (c + 1) * CHUNK],
-                in1=acc_of[(c, m)][:], op=ALU.add,
+        def multiply(b, g):
+            i, j, n = b // 8, b % 8 // 2, b % 2
+            cols = slice(i * CHUNK, (i + 1) * CHUNK)
+            if g == 0:
+                acc_of[b] = psum.tile([P, CHUNK], F32, name="acc", tag="bank")
+            unit = j * PASSES + g
+            nc.tensor.matmul_mx(
+                out=acc_of[b][:],
+                lhsT=vcodes[:, unit, n, :].bitcast(FP8X4),
+                lhsT_scale=vscl[:, unit, n, :],
+                rhs=wcodes[:, g, cols].bitcast(FP8X4),
+                rhs_scale=wscl[:, g, cols],
+                start=(g == 0),
+                stop=(g == PASSES - 1),
             )
 
-        def e2(c, m):
-            y = y_of[(c, m)]
-            ss = statp.tile([P, 4], F32, name="ss", tag="ss")
+        def add(b):
+            c = ORDER[b // 8]
+            y = yp.tile([P, CHUNK], F32, name="y", tag="y")
+            y_of[b] = y
+            nc.vector.tensor_tensor(
+                out=y[:], in0=bias_bc[:, c * CHUNK : (c + 1) * CHUNK],
+                in1=acc_of[b][:], op=ALU.add,
+            )
+
+        def square(b):
+            half = b % 2
+            if half == 0:
+                ss_of[b // 2] = statp.tile([P, 2, 4], F32, name="ss", tag="ss")
+            ss = ss_of[b // 2]
             for h in range(4):
                 junk = junkp.tile([P, HD], BF16, name="junk", tag="junk")
                 nc.scalar.activation(
-                    out=junk[:], in_=y[:, h * HD : (h + 1) * HD], func=ACT.Square,
-                    accum_out=ss[:, h : h + 1],
+                    out=junk[:], in_=y_of[b][:, h * HD : (h + 1) * HD], func=ACT.Square,
+                    accum_out=ss[:, half, h : h + 1],
                 )
-            rt = statp.tile([P, 4], F32, name="rt", tag="rt")
-            rt_of[(c, m)] = rt
-            nc.scalar.activation(
-                out=rt[:], in_=ss[:], func=ACT.Abs_reciprocal_sqrt, bias=eps_t[:], scale=1.0 / HD
-            )
+            if half == 1:
+                rt = statp.tile([P, 2, 4], F32, name="rt", tag="rt")
+                rt_of[b // 2] = rt
+                nc.scalar.activation(
+                    out=rt[:], in_=ss[:], func=ACT.Abs_reciprocal_sqrt, bias=eps_t[:],
+                    scale=1.0 / HD,
+                )
 
-        def e3(c, m):
-            y = y_of[(c, m)]
-            rstd = rt_of[(c, m)]
+        def scale(b):
+            y = y_of[b]
+            rt = rt_of[b // 2]
             for h in range(4):
                 hs = slice(h * HD, (h + 1) * HD)
                 nc.vector.scalar_tensor_tensor(
-                    out=y[:, hs], in0=y[:, hs], scalar=rstd[:, h : h + 1],
-                    in1=g_ps[:, c // 2, :], op0=ALU.mult, op1=ALU.mult,
+                    out=y[:, hs], in0=y[:, hs], scalar=rt[:, b % 2, h : h + 1],
+                    in1=g_ps[:, ORDER[b // 8] // 2, :], op0=ALU.mult, op1=ALU.mult,
                 )
 
-        def store(c, m):
-            j, n = m // 2, m % 2
+        def store(b):
+            c, j, n = ORDER[b // 8], b % 8 // 2, b % 2
             half = c % 2
             view = outs[c // 2].rearrange("n (j c) h d -> n j c (h d)", c=P)
             nc.sync.dma_start(
-                out=view[n, j, :, half * CHUNK : (half + 1) * CHUNK], in_=y_of[(c, m)][:]
+                out=view[n, j, :, half * CHUNK : (half + 1) * CHUNK], in_=y_of[b][:]
             )
 
-        for g in range(PASSES):
-            for t in range(4):
-                widen(0, g, t)
-            interleave(0, g)
-            if g >= 1:
-                quant_w(0, g - 1)
-        units = [(j, g) for j in range(4) for g in range(PASSES)]
-        vid_turn(*units[0])
-        vid_out(*units[0])
-        quant_w(0, PASSES - 1)
-        for i in range(1, len(units) + 1):
-            if i < len(units):
-                vid_turn(*units[i])
-                vid_out(*units[i])
-            j, g = units[i - 1]
-            vid_quant(j, g)
-            if g == PASSES - 1:
-                mm(0, 2 * j)
-                mm(0, 2 * j + 1)
-
-        banks = [(c, m) for c in ORDER for m in range(8)]
-        for i in range(NCHUNK):
-            c = ORDER[i]
-            items = prep_items(ORDER[i + 1]) if i + 1 < NCHUNK else []
-            pos = 0
-            for m in range(8):
-                e1(c, m)
-                if c < NORMED:
-                    e2(c, m)
-                else:
-                    store(c, m)
-                upto = min(len(items), ((m + 1) * len(items) + 7) // 8)
-                while pos < upto:
-                    items[pos]()
-                    pos += 1
-                if 8 * i + m >= LAG and banks[8 * i + m - LAG][0] < NORMED:
-                    e3(*banks[8 * i + m - LAG])
-                    store(*banks[8 * i + m - LAG])
-            if i + 1 < NCHUNK:
-                for m in range(8):
-                    mm(ORDER[i + 1], m)
-        for bank in banks[len(banks) - LAG :]:
-            if bank[0] < NORMED:
-                e3(*bank)
-                store(*bank)
+        steps = {
+            "widen": widen, "lay": lay, "quantize": quantize, "turn": turn, "empty": empty,
+            "vid_quantize": vid_quantize, "multiply": multiply, "add": add, "square": square,
+            "scale": scale, "store": store, "gains": spread_gains,
+        }
+        for step in make_plan():
+            steps[step[0]](*step[1:])

@@ -23,15 +23,15 @@ FLOPS = 2 * TOKENS * K * N
 
 WIDEN_ON_V = {(0, g, t) for g in (0, 1) for t in (0, 1)}
 G_FROM = 1
-OUT_ON_S = (1, 2)
+OUT_ON_S = (0, 1, 2)
 ORDER = (0, 1, 2, 4, 3, 5)
 NORMED = 4
-LAG = 6
+LAG = 8
 QUANT_EVERY = 5
-QUANT_FROM = 2
+QUANT_FROM = 1
 AHEAD = 7
-SETTLE = 3
-HEAD_PLANES = (3, 6, 9, 12)
+SETTLE = 4
+HEAD_PLANES = (4, 8, 12, 14)
 
 
 def make_plan():

@@ -22,6 +22,7 @@ EPS = 1e-6
 FLOPS = 2 * TOKENS * K * N
 
 WIDEN_ON_V = {(0, g, t) for g in (0, 1) for t in (0, 1)}
+G_BUFS = 1
 G_FROM = 1
 OUT_ON_S = (0, 1, 2)
 ORDER = (0, 1, 2, 4, 3, 5)
@@ -42,18 +43,26 @@ def make_plan():
     units = [(i, g) for i in range(1, NCHUNK) for g in range(PASSES)]
     at = {"plane": 0, "lay": 0, "quant": 0, "open": 0, "add": 0, "scale": 0, "pass": 0, "since": SETTLE}
     vid_parts = set()
+    unrooted = []
+    rooted = set()
     quantized = {(0, g) for g in range(PASSES)}
     done = {}
+
+    def root():
+        while unrooted:
+            plan.append(("rsqrt", unrooted[0]))
+            rooted.add(unrooted.pop(0))
 
     def widen_to(n):
         while at["plane"] < min(n, len(planes)):
             plan.append(("widen",) + planes[at["plane"]])
             at["plane"] += 1
+            root()
 
     def lay():
         while at["lay"] < len(units):
             u = at["lay"]
-            if 4 * (u + 1) > at["plane"] or (u > 0 and units[u - 1] not in quantized):
+            if 4 * (u + 1) > at["plane"] or (u >= G_BUFS and units[u - G_BUFS] not in quantized):
                 break
             plan.append(("lay",) + units[u])
             at["lay"] += 1
@@ -86,13 +95,18 @@ def make_plan():
         b = at["add"]
         waiting = sum(1 for n in normed if n < b) - at["scale"]
         can_add = b < banks and done.get(b, 0) == PASSES
-        can_scale = waiting > 0 and (normed[at["scale"]] | 1) < b
+        if b == banks:
+            root()
+        can_scale = waiting > 0 and normed[at["scale"]] // 2 in rooted
         settling = b % 8 == 0 and at["since"] < SETTLE
         if can_add and not (can_scale and (waiting >= LAG or settling)):
             plan.append(("add", b))
             at["add"] += 1
             if b in normed:
                 plan.append(("square", b))
+                root()
+                if b % 2 == 1:
+                    unrooted.append(b // 2)
             else:
                 plan.append(("store", b))
             multiply()
@@ -178,7 +192,7 @@ def tile_naswinattention_pa_kernel(
         vrawp = ctx.enter_context(tc.tile_pool(name="vrawp", bufs=8))
         widep = ctx.enter_context(tc.tile_pool(name="widep", bufs=8))
         grpp = ctx.enter_context(tc.tile_pool(name="grpp", bufs=3))
-        grpg = ctx.enter_context(tc.tile_pool(name="grpg", bufs=1))
+        grpg = ctx.enter_context(tc.tile_pool(name="grpg", bufs=G_BUFS))
         vgp = ctx.enter_context(tc.tile_pool(name="vgp", bufs=4))
         yp = ctx.enter_context(tc.tile_pool(name="yp", bufs=18))
         statp = ctx.enter_context(tc.tile_pool(name="statp", bufs=8))
@@ -364,13 +378,14 @@ def tile_naswinattention_pa_kernel(
                     out=junk[:], in_=y_of[b][:, h * HD : (h + 1) * HD], func=ACT.Square,
                     accum_out=ss[:, half, h : h + 1],
                 )
-            if half == 1:
-                rt = statp.tile([P, 2, 4], F32, name="rt", tag="rt")
-                rt_of[b // 2] = rt
-                nc.scalar.activation(
-                    out=rt[:], in_=ss[:], func=ACT.Abs_reciprocal_sqrt, bias=eps_t[:],
-                    scale=1.0 / HD,
-                )
+
+        def rsqrt(pair):
+            rt = statp.tile([P, 2, 4], F32, name="rt", tag="rt")
+            rt_of[pair] = rt
+            nc.scalar.activation(
+                out=rt[:], in_=ss_of[pair][:], func=ACT.Abs_reciprocal_sqrt, bias=eps_t[:],
+                scale=1.0 / HD,
+            )
 
         def scale(b):
             y = y_of[b]
@@ -393,7 +408,7 @@ def tile_naswinattention_pa_kernel(
         steps = {
             "widen": widen, "lay": lay, "quantize": quantize, "turn": turn, "empty": empty,
             "vid_quantize": vid_quantize, "multiply": multiply, "add": add, "square": square,
-            "scale": scale, "store": store, "gains": spread_gains,
+            "rsqrt": rsqrt, "scale": scale, "store": store, "gains": spread_gains,
         }
         for step in make_plan():
             steps[step[0]](*step[1:])

@@ -196,7 +196,7 @@ def tile_naswinattention_pa_kernel(
         vgp = ctx.enter_context(tc.tile_pool(name="vgp", bufs=4))
         yp = ctx.enter_context(tc.tile_pool(name="yp", bufs=18))
         statp = ctx.enter_context(tc.tile_pool(name="statp", bufs=8))
-        junkp = ctx.enter_context(tc.tile_pool(name="junkp", bufs=2))
+        junkp = ctx.enter_context(tc.tile_pool(name="junkp", bufs=16))
         psum = ctx.enter_context(tc.psum_pool(name="psum", bufs=7))
         gpp = ctx.enter_context(tc.psum_pool(name="gpp", bufs=1))
 

@@ -23,15 +23,16 @@ FLOPS = 2 * TOKENS * K * N
 
 WIDEN_ON_V = {(0, g, t) for g in (0, 1) for t in (0, 1)}
 G_BUFS = 1
-G_FROM = 1
-OUT_ON_S = (0, 1, 2)
+ON_G = {(i, g) for i in range(1, NCHUNK) for g in range(PASSES)} - {(1, 0)}
+LAST_ON_V = {(i, 0) for i in range(2, NCHUNK)}
+OUT_ON_S = (1, 2)
 ORDER = (0, 1, 2, 4, 3, 5)
 NORMED = 4
 LAG = 8
 QUANT_EVERY = 5
-QUANT_FROM = 1
+QUANT_FROM = 0
 AHEAD = 7
-SETTLE = 4
+SETTLE = 3
 HEAD_PLANES = (4, 8, 12, 14)
 
 
@@ -39,8 +40,10 @@ def make_plan():
     plan = []
     banks = TOKENS // P * NCHUNK
     normed = [b for b in range(banks) if ORDER[b // 8] < NORMED]
-    planes = [(i, g, t) for i in range(1, NCHUNK) for g in range(PASSES) for t in range(4)]
     units = [(i, g) for i in range(1, NCHUNK) for g in range(PASSES)]
+    planes = [u + (t,) for u in units for t in range(4) if t < 3 or u not in LAST_ON_V]
+    ready = {u: 1 + max(n for n, p in enumerate(planes) if p[:2] == u) for u in units}
+    last = set()
     at = {"plane": 0, "lay": 0, "quant": 0, "open": 0, "add": 0, "scale": 0, "pass": 0, "since": SETTLE}
     vid_parts = set()
     unrooted = []
@@ -62,7 +65,9 @@ def make_plan():
     def lay():
         while at["lay"] < len(units):
             u = at["lay"]
-            if 4 * (u + 1) > at["plane"] or (u >= G_BUFS and units[u - G_BUFS] not in quantized):
+            if ready[units[u]] > at["plane"] or (u >= G_BUFS and units[u - G_BUFS] not in quantized):
+                break
+            if units[u] in LAST_ON_V and units[u] not in last:
                 break
             plan.append(("lay",) + units[u])
             at["lay"] += 1
@@ -81,7 +86,11 @@ def make_plan():
 
     def quantize_next():
         i, g = units[at["quant"]]
-        widen_to(4 * (at["quant"] + 1))
+        widen_to(ready[i, g])
+        for u in units[at["quant"] : at["quant"] + 2]:
+            if u in LAST_ON_V and u not in last and ready[u] <= at["plane"]:
+                plan.append(("widen",) + u + (3,))
+                last.add(u)
         lay()
         plan.append(("quantize", i, g))
         quantized.add((i, g))
@@ -271,7 +280,7 @@ def tile_naswinattention_pa_kernel(
             wide = wide_of[(i, g)]
             half = c % 2
             src = wbytes[:, g, c // 2, t, half * CHUNK : (half + 1) * CHUNK].bitcast(FP8)
-            if (i, g, t) in WIDEN_ON_V:
+            if (i, g, t) in WIDEN_ON_V or (t == 3 and (i, g) in LAST_ON_V):
                 nc.vector.tensor_scalar(
                     out=wide[:, t, :], in0=src, scalar1=wsc[:, g, t : t + 1],
                     scalar2=None, op0=ALU.mult,
@@ -283,7 +292,7 @@ def tile_naswinattention_pa_kernel(
 
         def lay(i, g):
             src = wide_of[(i, g)][:].rearrange("p t n -> p n t")
-            if i >= G_FROM:
+            if (i, g) in ON_G:
                 grp = grpg.tile([P, CHUNK, 4], BF16, name="grpg", tag="grpg", align_bytes=64)
                 nc.gpsimd.tensor_scalar(
                     out=grp[:], in0=src, scalar1=1.0, scalar2=0.0, op0=ALU.mult, op1=ALU.add

@@ -21,19 +21,20 @@ HD = 128
 EPS = 1e-6
 FLOPS = 2 * TOKENS * K * N
 
-WIDEN_ON_V = {(0, g, t) for g in (0, 1) for t in (0, 1)}
+WIDEN_ON_V = {(0, g, t) for g in (0, 1) for t in range(4)}
+PAIRED = {(0, 0), (0, 1)}
 G_BUFS = 1
 ON_G = {(i, g) for i in range(1, NCHUNK) for g in range(PASSES)} - {(1, 0)}
-LAST_ON_V = {(i, 0) for i in range(2, NCHUNK)}
-OUT_ON_S = (1, 2)
+OUT_ON_V = {(2, 0), (3, 0)}
+EARLY = 4
 ORDER = (0, 1, 2, 4, 3, 5)
 NORMED = 4
 LAG = 8
 QUANT_EVERY = 5
 QUANT_FROM = 0
-AHEAD = 7
+AHEAD = 5
 SETTLE = 3
-HEAD_PLANES = (4, 8, 12, 14)
+HEAD_PLANES = (6, 9, 12, 14)
 
 
 def make_plan():
@@ -41,9 +42,7 @@ def make_plan():
     banks = TOKENS // P * NCHUNK
     normed = [b for b in range(banks) if ORDER[b // 8] < NORMED]
     units = [(i, g) for i in range(1, NCHUNK) for g in range(PASSES)]
-    planes = [u + (t,) for u in units for t in range(4) if t < 3 or u not in LAST_ON_V]
-    ready = {u: 1 + max(n for n, p in enumerate(planes) if p[:2] == u) for u in units}
-    last = set()
+    planes = [u + (t,) for u in units for t in range(4)]
     at = {"plane": 0, "lay": 0, "quant": 0, "open": 0, "add": 0, "scale": 0, "pass": 0, "since": SETTLE}
     vid_parts = set()
     unrooted = []
@@ -65,9 +64,7 @@ def make_plan():
     def lay():
         while at["lay"] < len(units):
             u = at["lay"]
-            if ready[units[u]] > at["plane"] or (u >= G_BUFS and units[u - G_BUFS] not in quantized):
-                break
-            if units[u] in LAST_ON_V and units[u] not in last:
+            if 4 * (u + 1) > at["plane"] or (u >= G_BUFS and units[u - G_BUFS] not in quantized):
                 break
             plan.append(("lay",) + units[u])
             at["lay"] += 1
@@ -86,11 +83,7 @@ def make_plan():
 
     def quantize_next():
         i, g = units[at["quant"]]
-        widen_to(ready[i, g])
-        for u in units[at["quant"] : at["quant"] + 2]:
-            if u in LAST_ON_V and u not in last and ready[u] <= at["plane"]:
-                plan.append(("widen",) + u + (3,))
-                last.add(u)
+        widen_to(4 * (at["quant"] + 1))
         lay()
         plan.append(("quantize", i, g))
         quantized.add((i, g))
@@ -130,6 +123,8 @@ def make_plan():
         return True
 
     for g in range(PASSES):
+        if g == PASSES - 1:
+            widen_to(EARLY)
         for t in range(4):
             plan.append(("widen", 0, g, t))
     for g in range(PASSES):
@@ -278,16 +273,22 @@ def tile_naswinattention_pa_kernel(
             if t == 0:
                 wide_of[(i, g)] = widep.tile([P, 4, CHUNK], BF16, name="wide", tag="wide")
             wide = wide_of[(i, g)]
+            if (i, g) in PAIRED:
+                dst = wide[:].rearrange("p t n -> p (t n)").rearrange(
+                    "p (u n e) -> p u n e", u=2, e=2
+                )[:, t // 2, :, t % 2]
+            else:
+                dst = wide[:, t, :]
             half = c % 2
             src = wbytes[:, g, c // 2, t, half * CHUNK : (half + 1) * CHUNK].bitcast(FP8)
-            if (i, g, t) in WIDEN_ON_V or (t == 3 and (i, g) in LAST_ON_V):
+            if (i, g, t) in WIDEN_ON_V:
                 nc.vector.tensor_scalar(
-                    out=wide[:, t, :], in0=src, scalar1=wsc[:, g, t : t + 1],
+                    out=dst, in0=src, scalar1=wsc[:, g, t : t + 1],
                     scalar2=None, op0=ALU.mult,
                 )
             else:
                 nc.scalar.activation(
-                    out=wide[:, t, :], in_=src, func=ACT.Copy, scale=wsc[:, g, t : t + 1]
+                    out=dst, in_=src, func=ACT.Copy, scale=wsc[:, g, t : t + 1]
                 )
 
         def lay(i, g):
@@ -299,7 +300,20 @@ def tile_naswinattention_pa_kernel(
                 )
             else:
                 grp = grpp.tile([P, CHUNK, 4], BF16, name="grp", tag="grp", align_bytes=64)
-                nc.vector.tensor_copy(out=grp[:], in_=src)
+            if (i, g) in PAIRED:
+                nc.vector.tensor_copy(
+                    out=grp[:].rearrange("p n t -> p (n t)").bitcast(F32).rearrange(
+                        "p (n u) -> p n u", u=2
+                    ),
+                    in_=wide_of[(i, g)][:].rearrange("p t n -> p (t n)").bitcast(F32).rearrange(
+                        "p (u n) -> p n u", u=2
+                    ),
+                )
+            elif (i, g) not in ON_G:
+                nc.vector.tensor_copy(
+                    out=grp[:].rearrange("p (c i) t -> p c t i", i=4),
+                    in_=src.rearrange("p (c i) t -> p c t i", i=4),
+                )
             grp_of[(i, g)] = grp
 
         def quantize(i, g):
@@ -331,10 +345,10 @@ def tile_naswinattention_pa_kernel(
             vg_of[(j, g)] = vg
             dst = vg[:].rearrange("p n (ac u) -> p n ac u", u=2)
             src = xt[:].rearrange("p n u a c -> p n (a c) u")
-            if g in OUT_ON_S:
-                nc.scalar.copy(out=dst, in_=src)
-            else:
+            if (j, g) in OUT_ON_V:
                 nc.vector.tensor_copy(out=dst, in_=src)
+            else:
+                nc.scalar.copy(out=dst, in_=src)
 
         def vid_quantize(j, g):
             unit = j * PASSES + g

from contextlib import ExitStack

import concourse.mybir as mybir
from concourse.masks import make_identity

F32 = mybir.dt.float32
BF16 = mybir.dt.bfloat16
U32 = mybir.dt.uint32
U8 = mybir.dt.uint8
FP8 = mybir.dt.float8_e4m3fn
FP8X4 = mybir.dt.float8_e4m3fn_x4
ACT = mybir.ActivationFunctionType
ALU = mybir.AluOpType

P = 128
TOKENS, K, N = 1024, 1536, 3072
PASSES = 3
CHUNK = 512
NCHUNK = 6
HD = 128
EPS = 1e-6
FLOPS = 2 * TOKENS * K * N

WIDEN_ON_V = {(0, g, t) for g in (0, 1) for t in range(4)}
PAIRED = {(0, 0), (0, 1)}
G_BUFS = 1
ON_G = {(i, g) for i in range(1, NCHUNK) for g in range(PASSES)} - {(1, 0)}
OUT_ON_V = {(2, 0), (3, 0)}
EARLY = 4
ORDER = (0, 1, 2, 4, 3, 5)
NORMED = 4
LAG = 8
QUANT_EVERY = 5
QUANT_FROM = 0
AHEAD = 5
SETTLE = 3
HEAD_PLANES = (6, 9, 12, 14)


def make_plan():
    plan = []
    banks = TOKENS // P * NCHUNK
    normed = [b for b in range(banks) if ORDER[b // 8] < NORMED]
    units = [(i, g) for i in range(1, NCHUNK) for g in range(PASSES)]
    planes = [u + (t,) for u in units for t in range(4)]
    at = {"plane": 0, "lay": 0, "quant": 0, "open": 0, "add": 0, "scale": 0, "pass": 0, "since": SETTLE}
    vid_parts = set()
    unrooted = []
    rooted = set()
    quantized = {(0, g) for g in range(PASSES)}
    done = {}

    def root():
        while unrooted:
            plan.append(("rsqrt", unrooted[0]))
            rooted.add(unrooted.pop(0))

    def widen_to(n):
        while at["plane"] < min(n, len(planes)):
            plan.append(("widen",) + planes[at["plane"]])
            at["plane"] += 1
            root()

    def lay():
        while at["lay"] < len(units):
            u = at["lay"]
            if 4 * (u + 1) > at["plane"] or (u >= G_BUFS and units[u - G_BUFS] not in quantized):
                break
            plan.append(("lay",) + units[u])
            at["lay"] += 1

    def multiply():
        while at["open"] < min(banks, at["add"] + AHEAD):
            b = at["open"]
            if (b // 8, 0) not in quantized or (b < 8 and b // 2 not in vid_parts):
                break
            done[b] = 0
            at["open"] += 1
        for b in range(at["open"]):
            while done[b] < PASSES and (b // 8, done[b]) in quantized:
                plan.append(("multiply", b, done[b]))
                done[b] += 1

    def quantize_next():
        i, g = units[at["quant"]]
        widen_to(4 * (at["quant"] + 1))
        lay()
        plan.append(("quantize", i, g))
        quantized.add((i, g))
        at["quant"] += 1
        if g == PASSES - 1:
            at["since"] = 0
        lay()
        multiply()

    def epilogue_pass():
        b = at["add"]
        waiting = sum(1 for n in normed if n < b) - at["scale"]
        can_add = b < banks and done.get(b, 0) == PASSES
        if b == banks:
            root()
        can_scale = waiting > 0 and normed[at["scale"]] // 2 in rooted
        settling = b % 8 == 0 and at["since"] < SETTLE
        if can_add and not (can_scale and (waiting >= LAG or settling)):
            plan.append(("add", b))
            at["add"] += 1
            if b in normed:
                plan.append(("square", b))
                root()
                if b % 2 == 1:
                    unrooted.append(b // 2)
            else:
                plan.append(("store", b))
            multiply()
        elif can_scale:
            plan.append(("scale", normed[at["scale"]]))
            plan.append(("store", normed[at["scale"]]))
            at["scale"] += 1
        else:
            return False
        at["pass"] += 1
        at["since"] += 1
        return True

    for g in range(PASSES):
        if g == PASSES - 1:
            widen_to(EARLY)
        for t in range(4):
            plan.append(("widen", 0, g, t))
    for g in range(PASSES):
        plan.append(("lay", 0, g))
        if g > 0:
            plan.append(("quantize", 0, g - 1))
    for g in range(PASSES):
        plan.append(("turn", 0, g))
    plan.append(("empty", 0, 0))
    plan.append(("turn", 1, 0))
    plan.append(("quantize", 0, PASSES - 1))
    for g in (1, 2):
        plan.append(("empty", 0, g))
        plan.append(("turn", 1, g))
    widen_to(HEAD_PLANES[0])
    plan.append(("vid_quantize", 0, 0))
    plan.append(("vid_quantize", 0, 1))
    plan.append(("empty", 1, 0))
    plan.append(("turn", 2, 0))
    plan.append(("vid_quantize", 0, 2))
    vid_parts.add(0)
    multiply()
    for g in (1, 2):
        plan.append(("empty", 1, g))
        plan.append(("turn", 2, g))
    widen_to(HEAD_PLANES[1])
    for g in range(PASSES):
        plan.append(("vid_quantize", 1, g))
    vid_parts.add(1)
    lay()
    multiply()
    for j in (2, 3):
        for g in range(PASSES):
            plan.append(("empty", j, g))
            if j == 2:
                plan.append(("turn", 3, g))
        widen_to(HEAD_PLANES[j])
        epilogue_pass()
        epilogue_pass()
        for g in range(PASSES):
            plan.append(("vid_quantize", j, g))
        vid_parts.add(j)
        if j == 2:
            quantize_next()
        multiply()
    plan.append(("gains",))

    at["pass"] = 0
    first = at["quant"]
    while at["add"] < banks or at["scale"] < len(normed):
        while at["quant"] < len(units) and (
            at["pass"] >= QUANT_FROM + QUANT_EVERY * (at["quant"] - first)
        ):
            quantize_next()
        if not epilogue_pass():
            quantize_next()
        widen_to(HEAD_PLANES[-1] + at["pass"])
        lay()
    return plan


def tile_naswinattention_pa_kernel(
    tc, vid, w_bytes, w_scale, bias, q_gain, k_gain, out_q, out_k, out_v
):
    nc = tc.nc
    with ExitStack() as ctx:
        ctx.enter_context(tc.manual_schedule())
        keep = ctx.enter_context(tc.tile_pool(name="keep", bufs=1))
        vrawp = ctx.enter_context(tc.tile_pool(name="vrawp", bufs=8))
        widep = ctx.enter_context(tc.tile_pool(name="widep", bufs=8))
        grpp = ctx.enter_context(tc.tile_pool(name="grpp", bufs=3))
        grpg = ctx.enter_context(tc.tile_pool(name="grpg", bufs=G_BUFS))
        vgp = ctx.enter_context(tc.tile_pool(name="vgp", bufs=4))
        yp = ctx.enter_context(tc.tile_pool(name="yp", bufs=18))
        statp = ctx.enter_context(tc.tile_pool(name="statp", bufs=8))
        junkp = ctx.enter_context(tc.tile_pool(name="junkp", bufs=16))
        psum = ctx.enter_context(tc.psum_pool(name="psum", bufs=7))
        gpp = ctx.enter_context(tc.psum_pool(name="gpp", bufs=1))

        wsc = keep.tile([P, PASSES, 4], F32, name="wsc")
        wbytes = keep.tile([P, PASSES, NCHUNK // 2, 4, 2 * CHUNK], U8, name="wbytes")
        wcodes = keep.tile([P, PASSES, N], U32, name="wcodes", align_bytes=64)
        wscl = keep.tile([P, PASSES, N], U8, name="wscl", align_bytes=64)
        vcodes = keep.tile([P, 12, 2, P], U32, name="vcodes", align_bytes=64)
        vscl = keep.tile([P, 12, 2, P], U8, name="vscl", align_bytes=64)
        bias_bc = keep.tile([P, N], BF16, name="bias_bc")
        g_bc = keep.tile([P, 2, HD], BF16, name="g_bc")
        ident_bf = keep.tile([P, P], BF16, name="ident_bf")
        g_ps = gpp.tile([P, 2, HD], F32, name="g_ps")
        ident = keep.tile([P, P], F32, name="ident")
        perm = keep.tile([P, P], F32, name="perm")
        eps_t = keep.tile([P, 1], F32, name="eps_t")
        warm = keep.tile([P, 1], F32, name="warm")

        w_view = w_bytes.rearrange("(g p t) n -> g p t n", p=P, t=4)

        def load_w(pair, g, t0=0, t1=4):
            nc.sync.dma_start(
                out=wbytes[:, g, pair, t0:t1, :],
                in_=w_view[g, :, t0:t1, pair * 2 * CHUNK : (pair + 1) * 2 * CHUNK],
            )

        vraw = []

        def load_vid(a):
            t = vrawp.tile([P, K], BF16, name="vraw", tag="vraw")
            nc.sync.dma_start(out=t[:], in_=vid[a * P : (a + 1) * P, :])
            vraw.append(t)

        nc.sync.dma_start(
            out=wsc[:], in_=w_scale.rearrange("(g p t) o -> p g (t o)", p=P, t=4)
        )
        load_w(0, 0, 0, 2)
        load_w(0, 0, 2, 4)
        load_w(0, 1)
        load_w(0, 2)
        for a in range(8):
            load_vid(a)
        nc.sync.dma_start(out=bias_bc[:], in_=bias.partition_broadcast(P))
        nc.sync.dma_start(out=g_bc[:, 0, :], in_=q_gain.partition_broadcast(P))
        nc.sync.dma_start(out=g_bc[:, 1, :], in_=k_gain.partition_broadcast(P))
        for pair in (1, 2):
            for g in range(PASSES):
                load_w(pair, g)

        nc.vector.memset(eps_t[:], EPS)
        nc.scalar.activation(out=warm[:], in_=eps_t[:], func=ACT.Abs_reciprocal_sqrt)
        make_identity(nc, ident[:])
        nc.vector.tensor_copy(
            out=perm[:].rearrange("p (n h w) -> p n h w", n=2, h=8, w=8),
            in_=ident[:].rearrange("p (h n w) -> p n h w", h=8, n=2, w=8),
        )
        nc.vector.tensor_copy(out=ident_bf[:], in_=ident[:])

        def spread_gains():
            nc.tensor.matmul(
                out=g_ps[:].rearrange("p a d -> p (a d)"), lhsT=ident_bf[:],
                rhs=g_bc[:].rearrange("p a d -> p (a d)"), start=True, stop=True,
            )

        wide_of = {}
        grp_of = {}

        def widen(i, g, t):
            c = ORDER[i]
            if t == 0:
                wide_of[(i, g)] = widep.tile([P, 4, CHUNK], BF16, name="wide", tag="wide")
            wide = wide_of[(i, g)]
            if (i, g) in PAIRED:
                dst = wide[:].rearrange("p t n -> p (t n)").rearrange(
                    "p (u n e) -> p u n e", u=2, e=2
                )[:, t // 2, :, t % 2]
            else:
                dst = wide[:, t, :]
            half = c % 2
            src = wbytes[:, g, c // 2, t, half * CHUNK : (half + 1) * CHUNK].bitcast(FP8)
            if (i, g, t) in WIDEN_ON_V:
                nc.vector.tensor_scalar(
                    out=dst, in0=src, scalar1=wsc[:, g, t : t + 1],
                    scalar2=None, op0=ALU.mult,
                )
            else:
                nc.scalar.activation(
                    out=dst, in_=src, func=ACT.Copy, scale=wsc[:, g, t : t + 1]
                )

        def lay(i, g):
            src = wide_of[(i, g)][:].rearrange("p t n -> p n t")
            if (i, g) in ON_G:
                grp = grpg.tile([P, CHUNK, 4], BF16, name="grpg", tag="grpg", align_bytes=64)
                nc.gpsimd.tensor_scalar(
                    out=grp[:], in0=src, scalar1=1.0, scalar2=0.0, op0=ALU.mult, op1=ALU.add
                )
            else:
                grp = grpp.tile([P, CHUNK, 4], BF16, name="grp", tag="grp", align_bytes=64)
            if (i, g) in PAIRED:
                nc.vector.tensor_copy(
                    out=grp[:].rearrange("p n t -> p (n t)").bitcast(F32).rearrange(
                        "p (n u) -> p n u", u=2
                    ),
                    in_=wide_of[(i, g)][:].rearrange("p t n -> p (t n)").bitcast(F32).rearrange(
                        "p (u n) -> p n u", u=2
                    ),
                )
            elif (i, g) not in ON_G:
                nc.vector.tensor_copy(
                    out=grp[:].rearrange("p (c i) t -> p c t i", i=4),
                    in_=src.rearrange("p (c i) t -> p c t i", i=4),
                )
            grp_of[(i, g)] = grp

        def quantize(i, g):
            cols = slice(i * CHUNK, (i + 1) * CHUNK)
            nc.vector.quantize_mx(
                out=wcodes[:, g, cols].bitcast(FP8X4),
                scales=wscl[:, g, cols],
                in_=grp_of[(i, g)][:].rearrange("p n t -> p (n t)"),
            )

        xt_of = {}
        vg_of = {}

        def turn(j, g):
            xt = psum.tile([P, 2, 2, 2, 64], F32, name="xt", tag="bank")
            xt_of[(j, g)] = xt
            for a2 in range(2):
                words = vraw[2 * j + a2][:].bitcast(F32)
                for u in range(2):
                    nc.tensor.transpose(
                        xt[:, :, u, a2, :],
                        words[:, 256 * g + u : 256 * (g + 1) : 2],
                        perm[:],
                    )

        def empty(j, g):
            xt = xt_of[(j, g)]
            vg = vgp.tile([P, 2, 256], F32, name="vg", tag="vg", align_bytes=64)
            vg_of[(j, g)] = vg
            dst = vg[:].rearrange("p n (ac u) -> p n ac u", u=2)
            src = xt[:].rearrange("p n u a c -> p n (a c) u")
            if (j, g) in OUT_ON_V:
                nc.vector.tensor_copy(out=dst, in_=src)
            else:
                nc.scalar.copy(out=dst, in_=src)

        def vid_quantize(j, g):
            unit = j * PASSES + g
            vg = vg_of[(j, g)]
            nc.vector.quantize_mx(
                out=vcodes[:, unit, :, :].rearrange("p n c -> p (n c)").bitcast(FP8X4),
                scales=vscl[:, unit, :, :].rearrange("p n c -> p (n c)"),
                in_=vg[:].rearrange("p n w -> p (n w)").bitcast(BF16),
            )

        acc_of = {}
        y_of = {}
        ss_of = {}
        rt_of = {}
        outs = (out_q, out_k, out_v)

        def multiply(b, g):
            i, j, n = b // 8, b % 8 // 2, b % 2
            cols = slice(i * CHUNK, (i + 1) * CHUNK)
            if g == 0:
                acc_of[b] = psum.tile([P, CHUNK], F32, name="acc", tag="bank")
            unit = j * PASSES + g
            nc.tensor.matmul_mx(
                out=acc_of[b][:],
                lhsT=vcodes[:, unit, n, :].bitcast(FP8X4),
                lhsT_scale=vscl[:, unit, n, :],
                rhs=wcodes[:, g, cols].bitcast(FP8X4),
                rhs_scale=wscl[:, g, cols],
                start=(g == 0),
                stop=(g == PASSES - 1),
            )

        def add(b):
            c = ORDER[b // 8]
            y = yp.tile([P, CHUNK], F32, name="y", tag="y")
            y_of[b] = y
            nc.vector.tensor_tensor(
                out=y[:], in0=bias_bc[:, c * CHUNK : (c + 1) * CHUNK],
                in1=acc_of[b][:], op=ALU.add,
            )

        def square(b):
            half = b % 2
            if half == 0:
                ss_of[b // 2] = statp.tile([P, 2, 4], F32, name="ss", tag="ss")
            ss = ss_of[b // 2]
            for h in range(4):
                junk = junkp.tile([P, HD], BF16, name="junk", tag="junk")
                nc.scalar.activation(
                    out=junk[:], in_=y_of[b][:, h * HD : (h + 1) * HD], func=ACT.Square,
                    accum_out=ss[:, half, h : h + 1],
                )

        def rsqrt(pair):
            rt = statp.tile([P, 2, 4], F32, name="rt", tag="rt")
            rt_of[pair] = rt
            nc.scalar.activation(
                out=rt[:], in_=ss_of[pair][:], func=ACT.Abs_reciprocal_sqrt, bias=eps_t[:],
                scale=1.0 / HD,
            )

        def scale(b):
            y = y_of[b]
            rt = rt_of[b // 2]
            for h in range(4):
                hs = slice(h * HD, (h + 1) * HD)
                nc.vector.scalar_tensor_tensor(
                    out=y[:, hs], in0=y[:, hs], scalar=rt[:, b % 2, h : h + 1],
                    in1=g_ps[:, ORDER[b // 8] // 2, :], op0=ALU.mult, op1=ALU.mult,
                )

        def store(b):
            c, j, n = ORDER[b // 8], b % 8 // 2, b % 2
            half = c % 2
            view = outs[c // 2].rearrange("n (j c) h d -> n j c (h d)", c=P)
            nc.sync.dma_start(
                out=view[n, j, :, half * CHUNK : (half + 1) * CHUNK], in_=y_of[b][:]
            )

        steps = {
            "widen": widen, "lay": lay, "quantize": quantize, "turn": turn, "empty": empty,
            "vid_quantize": vid_quantize, "multiply": multiply, "add": add, "square": square,
            "rsqrt": rsqrt, "scale": scale, "store": store, "gains": spread_gains,
        }
        for step in make_plan():
            steps[step[0]](*step[1:])
